import numpy as np
import ml_dtypes


def mxq(x, axis, fmt="e4m3"):
    dtype, down = {"e4m3": (ml_dtypes.float8_e4m3fn, 7), "e5m2": (ml_dtypes.float8_e5m2, 14)}[fmt]
    v = np.moveaxis(np.asarray(x, np.float32).astype(ml_dtypes.bfloat16).astype(np.float64), axis, -1)
    blocks = v.reshape(v.shape[:-1] + (-1, 32))
    amax = np.abs(blocks).max(-1, keepdims=True)
    byte = np.maximum(np.where(amax > 0, np.frexp(amax)[1] - 1 + 127, 0) - down, 1)
    scale = np.exp2(byte - 127.0)
    codes = (blocks / scale).astype(np.float32).astype(dtype).astype(np.float64)
    return np.moveaxis((codes * scale).reshape(v.shape), -1, axis)


WIDE = False


def mx_kscale(k):
    if not WIDE:
        return np.ones(k)
    levels = np.array([10, -10, 5, -5, 0])
    a = np.random.permutation(np.resize(levels, k // 512 * 4)).reshape(k // 512, 4)
    idx = np.arange(k)
    return np.exp2(a[idx // 512, idx % 128 // 32])


BF16 = ml_dtypes.bfloat16


def bf(x):
    return np.asarray(x, np.float32).astype(BF16)


def f64(x):
    return np.asarray(x).astype(np.float64)


E2M1 = np.array([0.0, 0.5, 1.0, 1.5, 2.0, 3.0, 4.0, 6.0, -0.0, -0.5, -1.0, -1.5, -2.0, -3.0, -4.0, -6.0])


def pack_weight(w, fmt):
    k, n = w.shape
    w = f64(bf(w)).reshape(k // 32, 32, n)
    amax = np.abs(w).max(1)
    if fmt == "e4m3":
        byte = np.frexp(amax)[1] - 1 + 127 - 7
    else:
        mant, ex = np.frexp(amax / 6.0)
        byte = np.where(mant > 0.5, ex, ex - 1) + 127
    byte = np.clip(np.where(amax > 0, byte, 1), 1, 254)
    scaled = (w * np.exp2(127.0 - byte)[:, None, :]).reshape(k, n).astype(np.float32)
    by_word = np.ascontiguousarray(scaled.reshape(k // 512, 128, 4, n).transpose(0, 1, 3, 2))
    if fmt == "e4m3":
        words = by_word.astype(ml_dtypes.float8_e4m3fn).view(np.uint8)
    else:
        c = by_word.astype(ml_dtypes.float4_e2m1fn).view(np.uint8) & 0xF
        words = c[..., 0::2] | (c[..., 1::2] << 4)
    return np.ascontiguousarray(words), np.ascontiguousarray(byte.astype(np.uint8).reshape(k // 512, 16, n))


def unpack_weight(words, scales, fmt):
    g, p, n, _ = words.shape
    if fmt == "e4m3":
        vals = np.ascontiguousarray(words).view(ml_dtypes.float8_e4m3fn).astype(np.float64)
    else:
        nib = np.empty((g, p, n, 4), np.uint8)
        nib[..., 0::2] = words & 0xF
        nib[..., 1::2] = words >> 4
        vals = E2M1[nib]
    vals = vals * np.repeat(np.exp2(scales.astype(np.float64) - 127.0), 8, axis=1)[..., None]
    return vals.transpose(0, 1, 3, 2).reshape(g * 512, n)


B, S, M, D, H = 8, 128, 16, 256, 1024
FMT = "e4m3"


def setup_inputs():
    s = mx_kscale(2 * D)
    lens = np.random.randint(0, M + 1, (B, S))
    valid = (np.arange(M)[None, None, :] < lens[:, :, None]).astype(np.float64)
    src = np.random.standard_normal((B, S, M, D)) / np.sqrt(M) * s[:D]
    neigh = np.random.standard_normal((B, S, M, D)) * 2.0 * valid[..., None] * s[D:]
    words, scales = pack_weight(np.random.standard_normal((2 * D, H)) / np.sqrt(2 * D) / s[:, None], FMT)
    return {"src_node_features": bf(src), "neigh_node_features": bf(neigh),
            "W_map_words": words, "W_map_scales": scales,
            "b_map": bf(-0.5 + 0.3 * np.random.standard_normal(H))}


def reference(src_node_features, neigh_node_features, W_map_words, W_map_scales, b_map):
    src, neigh = f64(src_node_features), f64(neigh_node_features)
    valid = np.any(neigh != 0, axis=-1)
    num = np.sum(valid, axis=-1).astype(np.float64)
    neigh_mean = neigh.sum(axis=2) / np.maximum(num, 1.0)[..., None]
    hidden = np.concatenate([src.sum(axis=2), neigh_mean], axis=-1)
    hidden = hidden.reshape(-1, hidden.shape[-1])
    v = (mxq(hidden, 1, "e4m3") @ unpack_weight(W_map_words, W_map_scales, FMT)) + f64(b_map)
    return np.where(v >= 0, v, 0.01 * v)

@@ -1,0 +1,237 @@
+from contextlib import ExitStack
+
+import concourse.mybir as mybir
+from concourse.masks import make_identity
+
+F32 = mybir.dt.float32
+BF16 = mybir.dt.bfloat16
+I32 = mybir.dt.int32
+U32 = mybir.dt.uint32
+U8 = mybir.dt.uint8
+FP8X4 = mybir.dt.float8_e4m3fn_x4
+ALU = mybir.AluOpType
+ACT = mybir.ActivationFunctionType
+AX = mybir.AxisListType
+
+P = 128
+PACK = 4
+NODE_TILES = 8
+SLOTS = 16
+FEAT = 256
+FEAT_BLOCKS = FEAT // P
+K = 2 * FEAT
+H = 1024
+N_TILE = 512
+GROUP = P // SLOTS
+GROUPS = P // GROUP
+SRC_P = FEAT // PACK
+NEG_SLOPE = 0.01
+
+FLOPS = 2 * NODE_TILES * P * K * H
+
+
+def tile_syntacticgcn_kernel(
+    tc, src_node_features, neigh_node_features, W_map_words, W_map_scales, b_map, out
+):
+    nc = tc.nc
+    with ExitStack() as ctx:
+        const = ctx.enter_context(tc.tile_pool(name="const", bufs=1))
+        inputs = ctx.enter_context(tc.tile_pool(name="inputs", bufs=1))
+        work = ctx.enter_context(tc.tile_pool(name="work", bufs=2))
+        results = ctx.enter_context(tc.tile_pool(name="results", bufs=NODE_TILES))
+        psum = ctx.enter_context(tc.psum_pool(name="psum", bufs=1))
+        ctx.enter_context(tc.manual_schedule())
+
+        w_scales = const.tile([P, H], U8, align_bytes=64)
+        nc.vector.memset(w_scales[:].bitcast(I32), 0)
+        ident = const.tile([P, P], BF16)
+        make_identity(nc, ident[:])
+        slot_sum_f32 = const.tile([P, GROUP], F32)
+        nc.vector.tensor_reduce(
+            out=slot_sum_f32[:],
+            in_=ident[:].rearrange("p (n m) -> p n m", m=SLOTS),
+            axis=AX.X,
+            op=ALU.add,
+        )
+        slot_sum = const.tile([P, GROUP], BF16)
+        nc.vector.tensor_copy(out=slot_sum[:], in_=slot_sum_f32[:])
+
+        neigh_tiles = []
+        src_tiles = []
+
+        def load_neigh(i):
+            neigh_tile = inputs.tile([P, SLOTS, FEAT], BF16, name="neigh%d" % i)
+            nc.sync.dma_start(out=neigh_tile[:], in_=neigh_node_features[i])
+            neigh_tiles.append(neigh_tile)
+
+        def load_src(i):
+            src_tile = inputs.tile([P, GROUPS, FEAT], BF16, name="src%d" % i)
+            rows = src_node_features[i].rearrange("s m d -> (s m) d")
+            nc.sync.dma_start(out=src_tile[:], in_=rows.rearrange("(g p) d -> p g d", p=P))
+            src_tiles.append(src_tile)
+
+        w_words = const.tile([P, PACK * H], U8, align_bytes=64)
+        bias_all = const.tile([P, H], BF16)
+
+        def load_weights():
+            for quadrant in range(4):
+                nc.sync.dma_start(
+                    out=w_scales[32 * quadrant : 32 * quadrant + 4, :].bitcast(I32),
+                    in_=W_map_scales[0, 4 * quadrant : 4 * quadrant + 4, :].bitcast(I32),
+                )
+            nc.sync.dma_start(
+                out=w_words[:].bitcast(I32),
+                in_=W_map_words[0].rearrange("p n t -> p (n t)").bitcast(I32),
+            )
+            nc.sync.dma_start(out=bias_all[:], in_=b_map.partition_broadcast(P))
+
+        load_neigh(0)
+        load_neigh(1)
+        load_src(0)
+        load_weights()
+        for i in range(2, NODE_TILES):
+            load_neigh(i)
+            load_src(i - 1)
+        load_src(NODE_TILES - 1)
+
+        neigh_sum_of = {}
+        count_of = {}
+        inv_count_of = {}
+        hidden_of = {}
+        grouped_of = {}
+        acc_of = {}
+
+        def invert_count(i):
+            at_least_one = work.tile([P, 1], F32)
+            nc.vector.tensor_scalar_max(out=at_least_one[:], in0=count_of[i][:], scalar1=1.0)
+            inv_count = work.tile([P, 1], F32)
+            nc.vector.reciprocal(out=inv_count[:], in_=at_least_one[:])
+            inv_count_of[i] = inv_count
+
+        def sum_neigh(i):
+            neigh_sum = work.tile([P, FEAT], F32)
+            nc.vector.tensor_reduce(
+                out=neigh_sum[:],
+                in_=neigh_tiles[i][:].rearrange("p m d -> p d m"),
+                axis=AX.X,
+                op=ALU.add,
+            )
+            neigh_sum_of[i] = neigh_sum
+
+        def count_neigh(i):
+            row_abs = work.tile([P, SLOTS], F32)
+            for m in range(SLOTS):
+                unused = work.tile([P, FEAT], BF16)
+                nc.scalar.activation(
+                    out=unused[:],
+                    in_=neigh_tiles[i][:, m, :],
+                    func=ACT.Abs,
+                    accum_out=row_abs[:, m : m + 1],
+                )
+            valid = work.tile([P, SLOTS], F32)
+            count = work.tile([P, 1], F32)
+            nc.scalar.activation(out=valid[:], in_=row_abs[:], func=ACT.Sign, accum_out=count[:])
+            count_of[i] = count
+
+        def sum_src(i):
+            a_t = psum.tile([P, FEAT_BLOCKS, P], F32, bufs=2)
+            for c in range(FEAT_BLOCKS):
+                for g in range(GROUPS):
+                    nc.tensor.matmul(
+                        out=a_t[:, c, g * GROUP : (g + 1) * GROUP],
+                        lhsT=src_tiles[i][:, g, c * P : (c + 1) * P],
+                        rhs=slot_sum[:],
+                        start=True,
+                        stop=True,
+                    )
+            a_t_bf = work.tile([P, FEAT_BLOCKS, P], BF16)
+            nc.scalar.copy(out=a_t_bf[:], in_=a_t[:])
+            a_rows = psum.tile([P, FEAT_BLOCKS, P], BF16)
+            for c in range(FEAT_BLOCKS):
+                nc.tensor.transpose(a_rows[:, c, :], a_t_bf[:, c, :], ident[:])
+            return a_rows
+
+        def scale_neigh(i):
+            nc.scalar.activation(
+                out=hidden_of[i][:, :, SRC_P:P],
+                in_=neigh_sum_of[i][:].rearrange("n (p t) -> n t p", t=PACK),
+                func=ACT.Copy,
+                scale=inv_count_of[i][:, 0:1],
+            )
+
+        def place_src(i, a_rows):
+            hidden = work.tile([P, PACK, P], BF16)
+            nc.scalar.copy(
+                out=hidden[:, :, 0:SRC_P],
+                in_=a_rows[:].rearrange("n c q -> n (c q)").rearrange("n (p t) -> n t p", t=PACK),
+            )
+            hidden_of[i] = hidden
+
+        def transpose_hidden(i):
+            hidden_t = psum.tile([P, PACK, P], BF16)
+            for t in range(PACK):
+                nc.tensor.transpose(hidden_t[:, t, :], hidden_of[i][:, t, :], ident[:])
+            grouped = work.tile([P, P, PACK], BF16, align_bytes=64)
+            nc.scalar.copy(out=grouped[:], in_=hidden_t[:].rearrange("p t n -> p n t"))
+            grouped_of[i] = grouped
+
+        def finish(i):
+            result = results.tile([P, H], F32)
+            for h in range(H // N_TILE):
+                cols = slice(h * N_TILE, (h + 1) * N_TILE)
+                nc.vector.tensor_tensor(
+                    out=result[:, cols], in0=acc_of[i][h][:], in1=bias_all[:, cols], op=ALU.add
+                )
+                nc.vector.scalar_tensor_tensor(
+                    out=result[:, cols],
+                    in0=result[:, cols],
+                    scalar=NEG_SLOPE,
+                    in1=result[:, cols],
+                    op0=ALU.mult,
+                    op1=ALU.max,
+                )
+            nc.sync.dma_start(out=out[i * P : (i + 1) * P, :], in_=result[:])
+
+        def quantise_and_multiply(i):
+            codes = work.tile([P, P], U32, align_bytes=64)
+            scales = work.tile([P, P], U8, align_bytes=64)
+            nc.vector.quantize_mx(
+                out=codes[:].bitcast(FP8X4),
+                scales=scales[:],
+                in_=grouped_of[i][:].rearrange("p n t -> p (n t)"),
+            )
+            banks = []
+            for h in range(H // N_TILE):
+                acc = psum.tile([P, N_TILE], F32, bufs=4)
+                nc.tensor.matmul_mx(
+                    out=acc[:],
+                    lhsT=codes[:].bitcast(FP8X4),
+                    lhsT_scale=scales[:],
+                    rhs=w_words[:, h * PACK * N_TILE : (h + 1) * PACK * N_TILE].bitcast(FP8X4),
+                    rhs_scale=w_scales[:, h * N_TILE : (h + 1) * N_TILE],
+                    start=True,
+                    stop=True,
+                )
+                banks.append(acc)
+            acc_of[i] = banks
+
+        def live(i):
+            return 0 <= i < NODE_TILES
+
+        for step in range(NODE_TILES + 3):
+            if live(step - 1):
+                invert_count(step - 1)
+            if live(step):
+                sum_neigh(step)
+                count_neigh(step)
+                a_rows = sum_src(step)
+            if live(step - 1):
+                scale_neigh(step - 1)
+            if live(step):
+                place_src(step, a_rows)
+            if live(step - 1):
+                transpose_hidden(step - 1)
+            if live(step - 3):
+                finish(step - 3)
+            if live(step - 2):
+                quantise_and_multiply(step - 2)

@@ -109,14 +109,23 @@ def tile_syntacticgcn_kernel(
             inv_count_of[i] = inv_count
 
         def sum_neigh(i):
-            neigh_sum = work.tile([P, FEAT], F32)
-            nc.vector.tensor_reduce(
-                out=neigh_sum[:],
-                in_=neigh_tiles[i][:].rearrange("p m d -> p d m"),
-                axis=AX.X,
+            width = SLOTS // 2
+            partial = work.tile([P, width, FEAT], F32)
+            nc.vector.tensor_tensor(
+                out=partial[:],
+                in0=neigh_tiles[i][:, 0:width, :],
+                in1=neigh_tiles[i][:, width : 2 * width, :],
                 op=ALU.add,
             )
-            neigh_sum_of[i] = neigh_sum
+            while width > 1:
+                width //= 2
+                nc.vector.tensor_tensor(
+                    out=partial[:, 0:width, :],
+                    in0=partial[:, 0:width, :],
+                    in1=partial[:, width : 2 * width, :],
+                    op=ALU.add,
+                )
+            neigh_sum_of[i] = partial
 
         def count_neigh(i):
             row_abs = work.tile([P, SLOTS], F32)
@@ -154,7 +163,7 @@ def tile_syntacticgcn_kernel(
         def scale_neigh(i):
             nc.scalar.activation(
                 out=hidden_of[i][:, :, SRC_P:P],
-                in_=neigh_sum_of[i][:].rearrange("n (p t) -> n t p", t=PACK),
+                in_=neigh_sum_of[i][:, 0, :].rearrange("n (p t) -> n t p", t=PACK),
                 func=ACT.Copy,
                 scale=inv_count_of[i][:, 0:1],
             )

@@ -40,7 +40,6 @@ def tile_syntacticgcn_kernel(
         work = ctx.enter_context(tc.tile_pool(name="work", bufs=2))
         results = ctx.enter_context(tc.tile_pool(name="results", bufs=NODE_TILES))
         psum = ctx.enter_context(tc.psum_pool(name="psum", bufs=1))
-        ctx.enter_context(tc.manual_schedule())
 
         w_scales = const.tile([P, H], U8, align_bytes=64)
         nc.vector.memset(w_scales[:].bitcast(I32), 0)

@@ -26,6 +26,7 @@ GROUP = P // SLOTS
 GROUPS = P // GROUP
 SRC_P = FEAT // PACK
 NEG_SLOPE = 0.01
+FIRST_LOAD_PIECES = 4
 
 FLOPS = 2 * NODE_TILES * P * K * H
 
@@ -60,7 +61,12 @@ def tile_syntacticgcn_kernel(
 
         def load_neigh(i):
             neigh_tile = inputs.tile([P, SLOTS, FEAT], BF16, name="neigh%d" % i)
-            nc.sync.dma_start(out=neigh_tile[:], in_=neigh_node_features[i])
+            pieces = FIRST_LOAD_PIECES if i == 0 else 1
+            step = SLOTS // pieces
+            for m in range(0, SLOTS, step):
+                nc.sync.dma_start(
+                    out=neigh_tile[:, m : m + step, :], in_=neigh_node_features[i][:, m : m + step, :]
+                )
             neigh_tiles.append(neigh_tile)
 
         def load_src(i):
@@ -93,29 +99,29 @@ def tile_syntacticgcn_kernel(
             load_src(i - 1)
         load_src(NODE_TILES - 1)
 
-        neigh_sum_of = {}
+        partial_of = {}
         count_of = {}
         inv_count_of = {}
+        a_t_of = {}
+        a_rows_of = {}
         hidden_of = {}
         grouped_of = {}
+        codes_of = {}
         acc_of = {}
 
-        def invert_count(i):
-            at_least_one = work.tile([P, 1], F32)
-            nc.vector.tensor_scalar_max(out=at_least_one[:], in0=count_of[i][:], scalar1=1.0)
-            inv_count = work.tile([P, 1], F32)
-            nc.vector.reciprocal(out=inv_count[:], in_=at_least_one[:])
-            inv_count_of[i] = inv_count
-
-        def sum_neigh(i):
-            width = SLOTS // 2
-            partial = work.tile([P, width, FEAT], F32)
+        def add_slot_halves(i):
+            partial = work.tile([P, SLOTS // 2, FEAT], F32)
             nc.vector.tensor_tensor(
                 out=partial[:],
-                in0=neigh_tiles[i][:, 0:width, :],
-                in1=neigh_tiles[i][:, width : 2 * width, :],
+                in0=neigh_tiles[i][:, 0 : SLOTS // 2, :],
+                in1=neigh_tiles[i][:, SLOTS // 2 : SLOTS, :],
                 op=ALU.add,
             )
+            partial_of[i] = partial
+
+        def finish_slot_sum(i):
+            partial = partial_of[i]
+            width = SLOTS // 2
             while width > 1:
                 width //= 2
                 nc.vector.tensor_tensor(
@@ -124,7 +130,6 @@ def tile_syntacticgcn_kernel(
                     in1=partial[:, width : 2 * width, :],
                     op=ALU.add,
                 )
-            neigh_sum_of[i] = partial
 
         def count_neigh(i):
             row_abs = work.tile([P, SLOTS], F32)
@@ -141,6 +146,25 @@ def tile_syntacticgcn_kernel(
             nc.scalar.activation(out=valid[:], in_=row_abs[:], func=ACT.Sign, accum_out=count[:])
             count_of[i] = count
 
+        def invert_count(i):
+            at_least_one = work.tile([P, 1], F32)
+            nc.vector.tensor_scalar_max(out=at_least_one[:], in0=count_of[i][:], scalar1=1.0)
+            inv_count = work.tile([P, 1], F32)
+            nc.vector.reciprocal(out=inv_count[:], in_=at_least_one[:])
+            inv_count_of[i] = inv_count
+
+        def place_neigh_mean(i):
+            hidden = work.tile([P, PACK, P], BF16)
+            nc.gpsimd.tensor_scalar(
+                out=hidden[:, :, SRC_P:P],
+                in0=partial_of[i][:, 0, :].rearrange("n (p t) -> n t p", t=PACK),
+                scalar1=inv_count_of[i][:, 0:1],
+                scalar2=0.0,
+                op0=ALU.mult,
+                op1=ALU.add,
+            )
+            hidden_of[i] = hidden
+
         def sum_src(i):
             a_t = psum.tile([P, FEAT_BLOCKS, P], F32, bufs=2)
             for c in range(FEAT_BLOCKS):
@@ -152,36 +176,61 @@ def tile_syntacticgcn_kernel(
                         start=True,
                         stop=True,
                     )
+            a_t_of[i] = a_t
+
+        def round_src_sum(i):
             a_t_bf = work.tile([P, FEAT_BLOCKS, P], BF16)
-            nc.scalar.copy(out=a_t_bf[:], in_=a_t[:])
+            nc.scalar.copy(out=a_t_bf[:], in_=a_t_of[i][:])
             a_rows = psum.tile([P, FEAT_BLOCKS, P], BF16)
             for c in range(FEAT_BLOCKS):
                 nc.tensor.transpose(a_rows[:, c, :], a_t_bf[:, c, :], ident[:])
-            return a_rows
+            a_rows_of[i] = a_rows
 
-        def scale_neigh(i):
-            nc.scalar.activation(
-                out=hidden_of[i][:, :, SRC_P:P],
-                in_=neigh_sum_of[i][:, 0, :].rearrange("n (p t) -> n t p", t=PACK),
-                func=ACT.Copy,
-                scale=inv_count_of[i][:, 0:1],
+        def place_src_sum(i):
+            nc.vector.tensor_copy(
+                out=hidden_of[i][:, :, 0:SRC_P],
+                in_=a_rows_of[i][:]
+                .rearrange("n c q -> n (c q)")
+                .rearrange("n (p t) -> n t p", t=PACK),
             )
-
-        def place_src(i, a_rows):
-            hidden = work.tile([P, PACK, P], BF16)
-            nc.scalar.copy(
-                out=hidden[:, :, 0:SRC_P],
-                in_=a_rows[:].rearrange("n c q -> n (c q)").rearrange("n (p t) -> n t p", t=PACK),
-            )
-            hidden_of[i] = hidden
 
         def transpose_hidden(i):
             hidden_t = psum.tile([P, PACK, P], BF16)
             for t in range(PACK):
                 nc.tensor.transpose(hidden_t[:, t, :], hidden_of[i][:, t, :], ident[:])
+            return hidden_t
+
+        def group_hidden(i, hidden_t):
             grouped = work.tile([P, P, PACK], BF16, align_bytes=64)
             nc.scalar.copy(out=grouped[:], in_=hidden_t[:].rearrange("p t n -> p n t"))
             grouped_of[i] = grouped
+
+        def quantise(i):
+            codes = work.tile([P, P], U32, align_bytes=64)
+            scales = work.tile([P, P], U8, align_bytes=64)
+            nc.vector.quantize_mx(
+                out=codes[:].bitcast(FP8X4),
+                scales=scales[:],
+                in_=grouped_of[i][:].rearrange("p n t -> p (n t)"),
+            )
+            codes_of[i] = (codes, scales)
+
+        def multiply(i):
+            codes, scales = codes_of[i]
+            banks = []
+            for h in range(H // N_TILE):
+                acc = psum.tile([P, N_TILE], F32, bufs=4)
+                nc.tensor.matmul_mx(
+                    out=acc[:],
+                    lhsT=codes[:].bitcast(FP8X4),
+                    lhsT_scale=scales[:],
+                    rhs=w_words[:, h * PACK * N_TILE : (h + 1) * PACK * N_TILE].bitcast(FP8X4),
+                    rhs_scale=w_scales[:, h * N_TILE : (h + 1) * N_TILE],
+                    start=True,
+                    stop=True,
+                )
+                banks.append(acc)
+            acc_of[i] = banks
 
         def finish(i):
             result = results.tile([P, H], F32)
@@ -198,48 +247,31 @@ def tile_syntacticgcn_kernel(
                     op0=ALU.mult,
                     op1=ALU.max,
                 )
-            nc.sync.dma_start(out=out[i * P : (i + 1) * P, :], in_=result[:])
-
-        def quantise_and_multiply(i):
-            codes = work.tile([P, P], U32, align_bytes=64)
-            scales = work.tile([P, P], U8, align_bytes=64)
-            nc.vector.quantize_mx(
-                out=codes[:].bitcast(FP8X4),
-                scales=scales[:],
-                in_=grouped_of[i][:].rearrange("p n t -> p (n t)"),
-            )
-            banks = []
-            for h in range(H // N_TILE):
-                acc = psum.tile([P, N_TILE], F32, bufs=4)
-                nc.tensor.matmul_mx(
-                    out=acc[:],
-                    lhsT=codes[:].bitcast(FP8X4),
-                    lhsT_scale=scales[:],
-                    rhs=w_words[:, h * PACK * N_TILE : (h + 1) * PACK * N_TILE].bitcast(FP8X4),
-                    rhs_scale=w_scales[:, h * N_TILE : (h + 1) * N_TILE],
-                    start=True,
-                    stop=True,
-                )
-                banks.append(acc)
-            acc_of[i] = banks
+                nc.sync.dma_start(out=out[i * P : (i + 1) * P, cols], in_=result[:, cols])
 
         def live(i):
             return 0 <= i < NODE_TILES
 
         for step in range(NODE_TILES + 3):
+            if live(step):
+                add_slot_halves(step)
+                count_neigh(step)
+            if live(step - 3):
+                quantise(step - 3)
+                multiply(step - 3)
+            if live(step):
+                finish_slot_sum(step)
             if live(step - 1):
                 invert_count(step - 1)
+                place_neigh_mean(step - 1)
+            if live(step - 2):
+                place_src_sum(step - 2)
+                hidden_t = transpose_hidden(step - 2)
             if live(step):
-                sum_neigh(step)
-                count_neigh(step)
-                a_rows = sum_src(step)
+                sum_src(step)
             if live(step - 1):
-                scale_neigh(step - 1)
-            if live(step):
-                place_src(step, a_rows)
-            if live(step - 1):
-                transpose_hidden(step - 1)
+                round_src_sum(step - 1)
+            if live(step - 2):
+                group_hidden(step - 2, hidden_t)
             if live(step - 3):
                 finish(step - 3)
-            if live(step - 2):
-                quantise_and_multiply(step - 2)

@@ -26,6 +26,8 @@ GROUP = P // SLOTS
 GROUPS = P // GROUP
 SRC_P = FEAT // PACK
 NEG_SLOPE = 0.01
+NEIGH_AHEAD = 3
+SRC_TILES_BEFORE_WEIGHTS = 2
 FIRST_LOAD_PIECES = 4
 
 FLOPS = 2 * NODE_TILES * P * K * H
@@ -88,16 +90,28 @@ def tile_syntacticgcn_kernel(
                 out=w_words[:].bitcast(I32),
                 in_=W_map_words[0].rearrange("p n t -> p (n t)").bitcast(I32),
             )
-            nc.sync.dma_start(out=bias_all[:], in_=b_map.partition_broadcast(P))
+
+        bias_row = const.tile([P, H], BF16)
+        nc.vector.memset(bias_row[:], 0.0)
+        ones = const.tile([P, P], BF16)
+        nc.vector.memset(ones[:], 1.0)
 
         load_neigh(0)
-        load_neigh(1)
-        load_src(0)
-        load_weights()
-        for i in range(2, NODE_TILES):
+        nc.sync.dma_start(out=bias_row[0:1, :], in_=b_map.unsqueeze(0))
+        for i in range(1, NEIGH_AHEAD):
             load_neigh(i)
-            load_src(i - 1)
-        load_src(NODE_TILES - 1)
+        for i in range(NODE_TILES):
+            load_src(i)
+            if i + NEIGH_AHEAD < NODE_TILES:
+                load_neigh(i + NEIGH_AHEAD)
+            if i == SRC_TILES_BEFORE_WEIGHTS - 1:
+                load_weights()
+
+        for h in range(H // N_TILE):
+            cols = slice(h * N_TILE, (h + 1) * N_TILE)
+            bias_bank = psum.tile([P, N_TILE], F32, tag="acc", bufs=4)
+            nc.tensor.matmul(out=bias_bank[:], lhsT=ones[:], rhs=bias_row[:, cols], start=True, stop=True)
+            nc.scalar.copy(out=bias_all[:, cols], in_=bias_bank[:])
 
         partial_of = {}
         count_of = {}
@@ -219,7 +233,7 @@ def tile_syntacticgcn_kernel(
             codes, scales = codes_of[i]
             banks = []
             for h in range(H // N_TILE):
-                acc = psum.tile([P, N_TILE], F32, bufs=4)
+                acc = psum.tile([P, N_TILE], F32, tag="acc", bufs=4)
                 nc.tensor.matmul_mx(
                     out=acc[:],
                     lhsT=codes[:].bitcast(FP8X4),

@@ -26,8 +26,6 @@ GROUP = P // SLOTS
 GROUPS = P // GROUP
 SRC_P = FEAT // PACK
 NEG_SLOPE = 0.01
-NEIGH_AHEAD = 3
-SRC_TILES_BEFORE_WEIGHTS = 2
 FIRST_LOAD_PIECES = 4
 
 FLOPS = 2 * NODE_TILES * P * K * H
@@ -90,28 +88,16 @@ def tile_syntacticgcn_kernel(
                 out=w_words[:].bitcast(I32),
                 in_=W_map_words[0].rearrange("p n t -> p (n t)").bitcast(I32),
             )
-
-        bias_row = const.tile([P, H], BF16)
-        nc.vector.memset(bias_row[:], 0.0)
-        ones = const.tile([P, P], BF16)
-        nc.vector.memset(ones[:], 1.0)
+            nc.sync.dma_start(out=bias_all[:], in_=b_map.partition_broadcast(P))
 
         load_neigh(0)
-        nc.sync.dma_start(out=bias_row[0:1, :], in_=b_map.unsqueeze(0))
-        for i in range(1, NEIGH_AHEAD):
+        load_neigh(1)
+        load_src(0)
+        load_weights()
+        for i in range(2, NODE_TILES):
             load_neigh(i)
-        for i in range(NODE_TILES):
-            load_src(i)
-            if i + NEIGH_AHEAD < NODE_TILES:
-                load_neigh(i + NEIGH_AHEAD)
-            if i == SRC_TILES_BEFORE_WEIGHTS - 1:
-                load_weights()
-
-        for h in range(H // N_TILE):
-            cols = slice(h * N_TILE, (h + 1) * N_TILE)
-            bias_bank = psum.tile([P, N_TILE], F32, tag="acc", bufs=4)
-            nc.tensor.matmul(out=bias_bank[:], lhsT=ones[:], rhs=bias_row[:, cols], start=True, stop=True)
-            nc.scalar.copy(out=bias_all[:, cols], in_=bias_bank[:])
+            load_src(i - 1)
+        load_src(NODE_TILES - 1)
 
         partial_of = {}
         count_of = {}
@@ -201,7 +187,7 @@ def tile_syntacticgcn_kernel(
             a_rows_of[i] = a_rows
 
         def place_src_sum(i):
-            nc.vector.tensor_copy(
+            nc.scalar.copy(
                 out=hidden_of[i][:, :, 0:SRC_P],
                 in_=a_rows_of[i][:]
                 .rearrange("n c q -> n (c q)")
@@ -233,7 +219,7 @@ def tile_syntacticgcn_kernel(
             codes, scales = codes_of[i]
             banks = []
             for h in range(H // N_TILE):
-                acc = psum.tile([P, N_TILE], F32, tag="acc", bufs=4)
+                acc = psum.tile([P, N_TILE], F32, bufs=4)
                 nc.tensor.matmul_mx(
                     out=acc[:],
                     lhsT=codes[:].bitcast(FP8X4),

@@ -27,6 +27,13 @@ GROUPS = P // GROUP
 SRC_P = FEAT // PACK
 NEG_SLOPE = 0.01
 FIRST_LOAD_PIECES = 4
+WORDS = FEAT // 2
+MAGNITUDE_BITS = 0x7FFF7FFF
+OR_STOP = 8
+
+NEIGH_ON_TENSOR = (1, 3, 5, 7)
+SCALAR_ROWS_TENSOR_TILE = 8
+SCALAR_ROWS_VECTOR_TILE = 16
 
 FLOPS = 2 * NODE_TILES * P * K * H
 
@@ -42,10 +49,15 @@ def tile_syntacticgcn_kernel(
         results = ctx.enter_context(tc.tile_pool(name="results", bufs=NODE_TILES))
         psum = ctx.enter_context(tc.psum_pool(name="psum", bufs=1))
 
+        def on_tensor(i):
+            return i in NEIGH_ON_TENSOR
+
         w_scales = const.tile([P, H], U8, align_bytes=64)
         nc.vector.memset(w_scales[:].bitcast(I32), 0)
         ident = const.tile([P, P], BF16)
         make_identity(nc, ident[:])
+        ident_f32 = const.tile([P, P], F32)
+        make_identity(nc, ident_f32[:])
         slot_sum_f32 = const.tile([P, GROUP], F32)
         nc.vector.tensor_reduce(
             out=slot_sum_f32[:],
@@ -55,24 +67,32 @@ def tile_syntacticgcn_kernel(
         )
         slot_sum = const.tile([P, GROUP], BF16)
         nc.vector.tensor_copy(out=slot_sum[:], in_=slot_sum_f32[:])
+        ones_col = const.tile([P, 1], BF16)
+        nc.vector.memset(ones_col[:], 1.0)
 
         neigh_tiles = []
         src_tiles = []
 
+        def load_by_slot(tile, features):
+            rows = features.rearrange("s m d -> (s m) d")
+            nc.sync.dma_start(out=tile[:], in_=rows.rearrange("(g p) d -> p g d", p=P))
+
         def load_neigh(i):
             neigh_tile = inputs.tile([P, SLOTS, FEAT], BF16, name="neigh%d" % i)
-            pieces = FIRST_LOAD_PIECES if i == 0 else 1
-            step = SLOTS // pieces
-            for m in range(0, SLOTS, step):
-                nc.sync.dma_start(
-                    out=neigh_tile[:, m : m + step, :], in_=neigh_node_features[i][:, m : m + step, :]
-                )
+            if on_tensor(i):
+                load_by_slot(neigh_tile, neigh_node_features[i])
+            else:
+                pieces = FIRST_LOAD_PIECES if i == 0 else 1
+                step = SLOTS // pieces
+                for m in range(0, SLOTS, step):
+                    nc.sync.dma_start(
+                        out=neigh_tile[:, m : m + step, :], in_=neigh_node_features[i][:, m : m + step, :]
+                    )
             neigh_tiles.append(neigh_tile)
 
         def load_src(i):
             src_tile = inputs.tile([P, GROUPS, FEAT], BF16, name="src%d" % i)
-            rows = src_node_features[i].rearrange("s m d -> (s m) d")
-            nc.sync.dma_start(out=src_tile[:], in_=rows.rearrange("(g p) d -> p g d", p=P))
+            load_by_slot(src_tile, src_node_features[i])
             src_tiles.append(src_tile)
 
         w_words = const.tile([P, PACK * H], U8, align_bytes=64)
@@ -100,14 +120,18 @@ def tile_syntacticgcn_kernel(
         load_src(NODE_TILES - 1)
 
         partial_of = {}
-        count_of = {}
+        or_of = {}
+        row_abs_of = {}
         inv_count_of = {}
-        a_t_of = {}
-        a_rows_of = {}
+        sum_t_of = {}
+        rows_of = {}
         hidden_of = {}
         grouped_of = {}
         codes_of = {}
         acc_of = {}
+
+        def scalar_rows(i):
+            return SCALAR_ROWS_TENSOR_TILE if on_tensor(i) else SCALAR_ROWS_VECTOR_TILE
 
         def add_slot_halves(i):
             partial = work.tile([P, SLOTS // 2, FEAT], F32)
@@ -131,68 +155,147 @@ def tile_syntacticgcn_kernel(
                     op=ALU.add,
                 )
 
-        def count_neigh(i):
+        def test_rows_scalar(i):
             row_abs = work.tile([P, SLOTS], F32)
-            for m in range(SLOTS):
+            for r in range(scalar_rows(i)):
                 unused = work.tile([P, FEAT], BF16)
                 nc.scalar.activation(
                     out=unused[:],
-                    in_=neigh_tiles[i][:, m, :],
+                    in_=neigh_tiles[i][:, r, :],
                     func=ACT.Abs,
-                    accum_out=row_abs[:, m : m + 1],
+                    accum_out=row_abs[:, r : r + 1],
                 )
-            valid = work.tile([P, SLOTS], F32)
-            count = work.tile([P, 1], F32)
-            nc.scalar.activation(out=valid[:], in_=row_abs[:], func=ACT.Sign, accum_out=count[:])
-            count_of[i] = count
+            row_abs_of[i] = row_abs
+
+        def or_row_halves(i):
+            first = scalar_rows(i)
+            if first == SLOTS:
+                return
+            words = (
+                neigh_tiles[i][:]
+                .rearrange("p r f -> p (r f)")
+                .bitcast(I32)
+                .rearrange("p (r w) -> p r w", w=WORDS)
+            )
+            ored = work.tile([P, SLOTS - first, WORDS // 2], I32)
+            nc.vector.tensor_tensor(
+                out=ored[:],
+                in0=words[:, first:SLOTS, 0 : WORDS // 2],
+                in1=words[:, first:SLOTS, WORDS // 2 : WORDS],
+                op=ALU.bitwise_or,
+            )
+            or_of[i] = ored
+
+        def finish_row_or(i):
+            first = scalar_rows(i)
+            if first == SLOTS:
+                return
+            ored = or_of[i]
+            width = WORDS // 2
+            while width > OR_STOP:
+                width //= 2
+                nc.vector.tensor_tensor(
+                    out=ored[:, :, 0:width],
+                    in0=ored[:, :, 0:width],
+                    in1=ored[:, :, width : 2 * width],
+                    op=ALU.bitwise_or,
+                )
+            nc.vector.tensor_scalar(
+                out=ored[:, :, 0:OR_STOP],
+                in0=ored[:, :, 0:OR_STOP],
+                scalar1=MAGNITUDE_BITS,
+                scalar2=None,
+                op0=ALU.bitwise_and,
+            )
+            nc.vector.tensor_reduce(
+                out=row_abs_of[i][:, first:SLOTS], in_=ored[:, :, 0:OR_STOP], axis=AX.X, op=ALU.max
+            )
 
         def invert_count(i):
             at_least_one = work.tile([P, 1], F32)
-            nc.vector.tensor_scalar_max(out=at_least_one[:], in0=count_of[i][:], scalar1=1.0)
+            if on_tensor(i):
+                masked = work.tile([P, GROUPS, GROUP], BF16)
+                nc.vector.scalar_tensor_tensor(
+                    out=masked[:],
+                    in0=row_abs_of[i][:].rearrange("q (g o) -> q g o", o=1).to_broadcast([P, GROUPS, GROUP]),
+                    scalar=0.0,
+                    in1=slot_sum[:].rearrange("q (o n) -> q o n", o=1).to_broadcast([P, GROUPS, GROUP]),
+                    op0=ALU.is_gt,
+                    op1=ALU.mult,
+                )
+                count_ps = psum.tile([P, 1], F32)
+                nc.tensor.matmul(
+                    out=count_ps[:],
+                    lhsT=masked[:].rearrange("q g n -> q (g n)"),
+                    rhs=ones_col[:],
+                    start=True,
+                    stop=True,
+                )
+                nc.vector.tensor_scalar_max(out=at_least_one[:], in0=count_ps[:], scalar1=1.0)
+            else:
+                valid = work.tile([P, SLOTS], F32)
+                count = work.tile([P, 1], F32)
+                nc.scalar.activation(out=valid[:], in_=row_abs_of[i][:], func=ACT.Sign, accum_out=count[:])
+                nc.vector.tensor_scalar_max(out=at_least_one[:], in0=count[:], scalar1=1.0)
             inv_count = work.tile([P, 1], F32)
             nc.vector.reciprocal(out=inv_count[:], in_=at_least_one[:])
             inv_count_of[i] = inv_count
 
-        def place_neigh_mean(i):
+        def new_hidden(i):
             hidden = work.tile([P, PACK, P], BF16)
+            hidden_of[i] = hidden
+
+        def place_neigh_mean_from_tree(i):
             nc.gpsimd.tensor_scalar(
-                out=hidden[:, :, SRC_P:P],
+                out=hidden_of[i][:, :, SRC_P:P],
                 in0=partial_of[i][:, 0, :].rearrange("n (p t) -> n t p", t=PACK),
                 scalar1=inv_count_of[i][:, 0:1],
                 scalar2=0.0,
                 op0=ALU.mult,
                 op1=ALU.add,
             )
-            hidden_of[i] = hidden
 
-        def sum_src(i):
-            a_t = psum.tile([P, FEAT_BLOCKS, P], F32, bufs=2)
-            for c in range(FEAT_BLOCKS):
-                for g in range(GROUPS):
-                    nc.tensor.matmul(
-                        out=a_t[:, c, g * GROUP : (g + 1) * GROUP],
-                        lhsT=src_tiles[i][:, g, c * P : (c + 1) * P],
-                        rhs=slot_sum[:],
-                        start=True,
-                        stop=True,
-                    )
-            a_t_of[i] = a_t
+        def sum_on_tensor(i):
+            sum_t = psum.tile([P, 2 * FEAT_BLOCKS, P], F32, bufs=2)
+            tiles = [src_tiles[i]] + ([neigh_tiles[i]] if on_tensor(i) else [])
+            for which, tile in enumerate(tiles):
+                for c in range(FEAT_BLOCKS):
+                    for g in range(GROUPS):
+                        nc.tensor.matmul(
+                            out=sum_t[:, which * FEAT_BLOCKS + c, g * GROUP : (g + 1) * GROUP],
+                            lhsT=tile[:, g, c * P : (c + 1) * P],
+                            rhs=slot_sum[:],
+                            start=True,
+                            stop=True,
+                        )
+            sum_t_of[i] = sum_t
 
-        def round_src_sum(i):
-            a_t_bf = work.tile([P, FEAT_BLOCKS, P], BF16)
-            nc.scalar.copy(out=a_t_bf[:], in_=a_t_of[i][:])
-            a_rows = psum.tile([P, FEAT_BLOCKS, P], BF16)
-            for c in range(FEAT_BLOCKS):
-                nc.tensor.transpose(a_rows[:, c, :], a_t_bf[:, c, :], ident[:])
-            a_rows_of[i] = a_rows
+        def blocks_on_tensor(i):
+            return 2 * FEAT_BLOCKS if on_tensor(i) else FEAT_BLOCKS
 
-        def place_src_sum(i):
+        def sums_to_rows(i):
+            blocks = blocks_on_tensor(i)
+            sum_sb = work.tile([P, 2 * FEAT_BLOCKS, P], F32)
+            nc.scalar.copy(out=sum_sb[:, 0:blocks, :], in_=sum_t_of[i][:, 0:blocks, :])
+            rows = psum.tile([P, 2 * FEAT_BLOCKS, P], F32)
+            for c in range(blocks):
+                nc.tensor.transpose(rows[:, c, :], sum_sb[:, c, :], ident_f32[:])
+            rows_of[i] = rows
+
+        def by_pack(rows_half):
+            return rows_half.rearrange("n c q -> n (c q)").rearrange("n (p t) -> n t p", t=PACK)
+
+        def place_from_rows(i):
             nc.scalar.copy(
-                out=hidden_of[i][:, :, 0:SRC_P],
-                in_=a_rows_of[i][:]
-                .rearrange("n c q -> n (c q)")
-                .rearrange("n (p t) -> n t p", t=PACK),
+                out=hidden_of[i][:, :, 0:SRC_P], in_=by_pack(rows_of[i][:, 0:FEAT_BLOCKS, :])
             )
+            if on_tensor(i):
+                nc.scalar.activation(
+                    out=hidden_of[i][:, :, SRC_P:P],
+                    in_=by_pack(rows_of[i][:, FEAT_BLOCKS : 2 * FEAT_BLOCKS, :]),
+                    func=ACT.Copy,
+                    scale=inv_count_of[i][:, 0:1],
+                )
 
         def transpose_hidden(i):
             hidden_t = psum.tile([P, PACK, P], BF16)
@@ -219,7 +322,7 @@ def tile_syntacticgcn_kernel(
             codes, scales = codes_of[i]
             banks = []
             for h in range(H // N_TILE):
-                acc = psum.tile([P, N_TILE], F32, bufs=4)
+                acc = psum.tile([P, N_TILE], F32, bufs=3)
                 nc.tensor.matmul_mx(
                     out=acc[:],
                     lhsT=codes[:].bitcast(FP8X4),
@@ -254,23 +357,31 @@ def tile_syntacticgcn_kernel(
 
         for step in range(NODE_TILES + 3):
             if live(step):
-                add_slot_halves(step)
-                count_neigh(step)
+                if on_tensor(step):
+                    or_row_halves(step)
+                else:
+                    add_slot_halves(step)
+                test_rows_scalar(step)
             if live(step - 3):
                 quantise(step - 3)
                 multiply(step - 3)
             if live(step):
-                finish_slot_sum(step)
+                if on_tensor(step):
+                    finish_row_or(step)
+                else:
+                    finish_slot_sum(step)
             if live(step - 1):
                 invert_count(step - 1)
-                place_neigh_mean(step - 1)
+                new_hidden(step - 1)
+                if not on_tensor(step - 1):
+                    place_neigh_mean_from_tree(step - 1)
             if live(step - 2):
-                place_src_sum(step - 2)
+                place_from_rows(step - 2)
                 hidden_t = transpose_hidden(step - 2)
             if live(step):
-                sum_src(step)
+                sum_on_tensor(step)
             if live(step - 1):
-                round_src_sum(step - 1)
+                sums_to_rows(step - 1)
             if live(step - 2):
                 group_hidden(step - 2, hidden_t)
             if live(step - 3):

@@ -18,7 +18,6 @@ PACK = 4
 NODE_TILES = 8
 SLOTS = 16
 FEAT = 256
-FEAT_BLOCKS = FEAT // P
 K = 2 * FEAT
 H = 1024
 N_TILE = 512
@@ -31,9 +30,11 @@ WORDS = FEAT // 2
 MAGNITUDE_BITS = 0x7FFF7FFF
 OR_STOP = 8
 
-NEIGH_ON_TENSOR = (1, 3, 5, 7)
-SCALAR_ROWS_TENSOR_TILE = 8
-SCALAR_ROWS_VECTOR_TILE = 16
+VECTOR_TILES = (0, 1)
+SCALAR_ROWS = (16, 16, 16, 16, 16, 8, 8, 8)
+
+GROUP_COPY_AFTER = 12
+LATE_TILE_ROUND = 3
 
 FLOPS = 2 * NODE_TILES * P * K * H
 
@@ -49,8 +50,8 @@ def tile_syntacticgcn_kernel(
         results = ctx.enter_context(tc.tile_pool(name="results", bufs=NODE_TILES))
         psum = ctx.enter_context(tc.psum_pool(name="psum", bufs=1))
 
-        def on_tensor(i):
-            return i in NEIGH_ON_TENSOR
+        def on_vector(i):
+            return i in VECTOR_TILES
 
         w_scales = const.tile([P, H], U8, align_bytes=64)
         nc.vector.memset(w_scales[:].bitcast(I32), 0)
@@ -69,31 +70,37 @@ def tile_syntacticgcn_kernel(
         nc.vector.tensor_copy(out=slot_sum[:], in_=slot_sum_f32[:])
         ones_col = const.tile([P, 1], BF16)
         nc.vector.memset(ones_col[:], 1.0)
+        factor_rows = []
+        for j in range(2):
+            factor_row = const.tile([P, P], F32, name="factor_rows%d" % j)
+            nc.gpsimd.memset(factor_row[:], 1.0)
+            factor_rows.append(factor_row)
 
-        neigh_tiles = []
-        src_tiles = []
+        neigh_tiles = {}
+        src_tiles = {}
+        both_tiles = {}
 
-        def load_by_slot(tile, features):
-            rows = features.rearrange("s m d -> (s m) d")
-            nc.sync.dma_start(out=tile[:], in_=rows.rearrange("(g p) d -> p g d", p=P))
+        def by_slot(features):
+            return features.rearrange("s m d -> (s m) d").rearrange("(g p) d -> p g d", p=P)
 
-        def load_neigh(i):
-            neigh_tile = inputs.tile([P, SLOTS, FEAT], BF16, name="neigh%d" % i)
-            if on_tensor(i):
-                load_by_slot(neigh_tile, neigh_node_features[i])
-            else:
+        def load(i):
+            if on_vector(i):
+                neigh_tile = inputs.tile([P, SLOTS, FEAT], BF16, name="neigh%d" % i)
                 pieces = FIRST_LOAD_PIECES if i == 0 else 1
                 step = SLOTS // pieces
                 for m in range(0, SLOTS, step):
                     nc.sync.dma_start(
                         out=neigh_tile[:, m : m + step, :], in_=neigh_node_features[i][:, m : m + step, :]
                     )
-            neigh_tiles.append(neigh_tile)
-
-        def load_src(i):
-            src_tile = inputs.tile([P, GROUPS, FEAT], BF16, name="src%d" % i)
-            load_by_slot(src_tile, src_node_features[i])
-            src_tiles.append(src_tile)
+                neigh_tiles[i] = neigh_tile
+                src_tile = inputs.tile([P, SLOTS, FEAT], BF16, name="src%d" % i)
+                nc.sync.dma_start(out=src_tile[:], in_=src_node_features[i])
+                src_tiles[i] = src_tile
+            else:
+                both = inputs.tile([P, GROUPS, K], BF16, name="both%d" % i)
+                nc.sync.dma_start(out=both[:, :, FEAT:K], in_=by_slot(neigh_node_features[i]))
+                nc.sync.dma_start(out=both[:, :, 0:FEAT], in_=by_slot(src_node_features[i]))
+                both_tiles[i] = both
 
         w_words = const.tile([P, PACK * H], U8, align_bytes=64)
         bias_all = const.tile([P, H], BF16)
@@ -110,73 +117,75 @@ def tile_syntacticgcn_kernel(
             )
             nc.sync.dma_start(out=bias_all[:], in_=b_map.partition_broadcast(P))
 
-        load_neigh(0)
-        load_neigh(1)
-        load_src(0)
+        load(0)
+        load(1)
+        load(2)
         load_weights()
-        for i in range(2, NODE_TILES):
-            load_neigh(i)
-            load_src(i - 1)
-        load_src(NODE_TILES - 1)
+        for i in range(3, NODE_TILES):
+            load(i)
 
         partial_of = {}
         or_of = {}
         row_abs_of = {}
         inv_count_of = {}
-        sum_t_of = {}
-        rows_of = {}
-        hidden_of = {}
+        factor_of = {}
+        hidden_ps_of = {}
         grouped_of = {}
         codes_of = {}
         acc_of = {}
 
-        def scalar_rows(i):
-            return SCALAR_ROWS_TENSOR_TILE if on_tensor(i) else SCALAR_ROWS_VECTOR_TILE
+        def neigh_row(i, r):
+            if on_vector(i):
+                return neigh_tiles[i][:, r, :]
+            return both_tiles[i][:, r, FEAT:K]
 
-        def add_slot_halves(i):
-            partial = work.tile([P, SLOTS // 2, FEAT], F32)
-            nc.vector.tensor_tensor(
-                out=partial[:],
-                in0=neigh_tiles[i][:, 0 : SLOTS // 2, :],
-                in1=neigh_tiles[i][:, SLOTS // 2 : SLOTS, :],
-                op=ALU.add,
-            )
-            partial_of[i] = partial
+        def add_slot_quarters(i, which):
+            tile = (src_tiles if which == 0 else neigh_tiles)[i]
+            partial = work.tile([P, SLOTS // 2, FEAT], F32, name="partial%d" % which)
+            quarter = SLOTS // 4
+            for half in range(2):
+                first = 2 * half * quarter
+                nc.vector.tensor_tensor(
+                    out=partial[:, half * quarter : (half + 1) * quarter, :],
+                    in0=tile[:, first : first + quarter, :],
+                    in1=tile[:, first + quarter : first + 2 * quarter, :],
+                    op=ALU.add,
+                )
+            partial_of[(i, which)] = partial
 
-        def finish_slot_sum(i):
-            partial = partial_of[i]
+        def finish_slot_sums(i):
             width = SLOTS // 2
             while width > 1:
                 width //= 2
-                nc.vector.tensor_tensor(
-                    out=partial[:, 0:width, :],
-                    in0=partial[:, 0:width, :],
-                    in1=partial[:, width : 2 * width, :],
-                    op=ALU.add,
-                )
+                for which in (1, 0):
+                    partial = partial_of[(i, which)]
+                    nc.vector.tensor_tensor(
+                        out=partial[:, 0:width, :],
+                        in0=partial[:, 0:width, :],
+                        in1=partial[:, width : 2 * width, :],
+                        op=ALU.add,
+                    )
 
-        def test_rows_scalar(i):
-            row_abs = work.tile([P, SLOTS], F32)
-            for r in range(scalar_rows(i)):
+        def test_rows_scalar(i, first, last):
+            if first == 0:
+                row_abs = work.tile([P, SLOTS], F32, bufs=3)
+                row_abs_of[i] = row_abs
+            for r in range(first, min(last, SCALAR_ROWS[i])):
                 unused = work.tile([P, FEAT], BF16)
                 nc.scalar.activation(
-                    out=unused[:],
-                    in_=neigh_tiles[i][:, r, :],
-                    func=ACT.Abs,
-                    accum_out=row_abs[:, r : r + 1],
+                    out=unused[:], in_=neigh_row(i, r), func=ACT.Abs, accum_out=row_abs_of[i][:, r : r + 1]
                 )
-            row_abs_of[i] = row_abs
 
         def or_row_halves(i):
-            first = scalar_rows(i)
+            first = SCALAR_ROWS[i]
             if first == SLOTS:
                 return
-            words = (
-                neigh_tiles[i][:]
-                .rearrange("p r f -> p (r f)")
-                .bitcast(I32)
-                .rearrange("p (r w) -> p r w", w=WORDS)
-            )
+            if on_vector(i):
+                words = neigh_tiles[i][:].rearrange("p r f -> p (r f)").bitcast(I32)
+                words = words.rearrange("p (r w) -> p r w", w=WORDS)
+            else:
+                words = both_tiles[i][:].rearrange("p r f -> p (r f)").bitcast(I32)
+                words = words.rearrange("p (r w) -> p r w", w=2 * WORDS)[:, :, WORDS : 2 * WORDS]
             ored = work.tile([P, SLOTS - first, WORDS // 2], I32)
             nc.vector.tensor_tensor(
                 out=ored[:],
@@ -187,7 +196,7 @@ def tile_syntacticgcn_kernel(
             or_of[i] = ored
 
         def finish_row_or(i):
-            first = scalar_rows(i)
+            first = SCALAR_ROWS[i]
             if first == SLOTS:
                 return
             ored = or_of[i]
@@ -213,7 +222,12 @@ def tile_syntacticgcn_kernel(
 
         def invert_count(i):
             at_least_one = work.tile([P, 1], F32)
-            if on_tensor(i):
+            if on_vector(i):
+                valid = work.tile([P, SLOTS], F32)
+                count = work.tile([P, 1], F32)
+                nc.scalar.activation(out=valid[:], in_=row_abs_of[i][:], func=ACT.Sign, accum_out=count[:])
+                nc.vector.tensor_scalar_max(out=at_least_one[:], in0=count[:], scalar1=1.0)
+            else:
                 masked = work.tile([P, GROUPS, GROUP], BF16)
                 nc.vector.scalar_tensor_tensor(
                     out=masked[:],
@@ -232,80 +246,75 @@ def tile_syntacticgcn_kernel(
                     stop=True,
                 )
                 nc.vector.tensor_scalar_max(out=at_least_one[:], in0=count_ps[:], scalar1=1.0)
+            if on_vector(i):
+                inv_count = const.tile([P, 1], F32, name="inv_count_kept%d" % i)
             else:
-                valid = work.tile([P, SLOTS], F32)
-                count = work.tile([P, 1], F32)
-                nc.scalar.activation(out=valid[:], in_=row_abs_of[i][:], func=ACT.Sign, accum_out=count[:])
-                nc.vector.tensor_scalar_max(out=at_least_one[:], in0=count[:], scalar1=1.0)
-            inv_count = work.tile([P, 1], F32)
+                inv_count = work.tile([P, 1], F32)
             nc.vector.reciprocal(out=inv_count[:], in_=at_least_one[:])
             inv_count_of[i] = inv_count
 
-        def new_hidden(i):
-            hidden = work.tile([P, PACK, P], BF16)
-            hidden_of[i] = hidden
+        def spread_factor(i):
+            factor_row = factor_rows[i % 2]
+            nc.vector.tensor_copy(
+                out=factor_row[:, SRC_P:P], in_=inv_count_of[i][:, 0:1].to_broadcast([P, P - SRC_P])
+            )
+            factor_ps = psum.tile([P, P], F32)
+            nc.tensor.transpose(factor_ps[:], factor_row[:], ident_f32[:])
+            factor = work.tile([P, P], F32)
+            nc.vector.tensor_copy(out=factor[:], in_=factor_ps[:])
+            factor_of[i] = factor
 
-        def place_neigh_mean_from_tree(i):
+        def sum_on_tensor(i, half):
+            if half == 0:
+                hidden_ps = psum.tile([P, PACK, P], F32, bufs=2)
+                hidden_ps_of[i] = hidden_ps
+            hidden_ps = hidden_ps_of[i]
+            for t in range(half * PACK // 2, (half + 1) * PACK // 2):
+                for g in range(GROUPS):
+                    nc.tensor.matmul(
+                        out=hidden_ps[:, t, g * GROUP : (g + 1) * GROUP],
+                        lhsT=both_tiles[i][:, g, t:K:PACK],
+                        rhs=slot_sum[:],
+                        start=True,
+                        stop=True,
+                    )
+
+        def scale_and_group(i):
+            grouped = work.tile([P, P, PACK], BF16, align_bytes=64)
+            nc.vector.tensor_tensor(
+                out=grouped[:],
+                in0=hidden_ps_of[i][:].rearrange("p t n -> p n t"),
+                in1=factor_of[i][:].rearrange("p (n o) -> p n o", o=1).to_broadcast([P, P, PACK]),
+                op=ALU.mult,
+            )
+            grouped_of[i] = grouped
+
+        def rows_to_hidden_ps(i):
+            hidden = work.tile([P, PACK, P], BF16)
             nc.gpsimd.tensor_scalar(
-                out=hidden_of[i][:, :, SRC_P:P],
-                in0=partial_of[i][:, 0, :].rearrange("n (p t) -> n t p", t=PACK),
+                out=hidden[:, :, 0:SRC_P],
+                in0=partial_of[(i, 0)][:, 0, :].rearrange("n (p t) -> n t p", t=PACK),
+                scalar1=1.0,
+                scalar2=0.0,
+                op0=ALU.mult,
+                op1=ALU.add,
+            )
+            nc.gpsimd.tensor_scalar(
+                out=hidden[:, :, SRC_P:P],
+                in0=partial_of[(i, 1)][:, 0, :].rearrange("n (p t) -> n t p", t=PACK),
                 scalar1=inv_count_of[i][:, 0:1],
                 scalar2=0.0,
                 op0=ALU.mult,
                 op1=ALU.add,
             )
-
-        def sum_on_tensor(i):
-            sum_t = psum.tile([P, 2 * FEAT_BLOCKS, P], F32, bufs=2)
-            tiles = [src_tiles[i]] + ([neigh_tiles[i]] if on_tensor(i) else [])
-            for which, tile in enumerate(tiles):
-                for c in range(FEAT_BLOCKS):
-                    for g in range(GROUPS):
-                        nc.tensor.matmul(
-                            out=sum_t[:, which * FEAT_BLOCKS + c, g * GROUP : (g + 1) * GROUP],
-                            lhsT=tile[:, g, c * P : (c + 1) * P],
-                            rhs=slot_sum[:],
-                            start=True,
-                            stop=True,
-                        )
-            sum_t_of[i] = sum_t
-
-        def blocks_on_tensor(i):
-            return 2 * FEAT_BLOCKS if on_tensor(i) else FEAT_BLOCKS
-
-        def sums_to_rows(i):
-            blocks = blocks_on_tensor(i)
-            sum_sb = work.tile([P, 2 * FEAT_BLOCKS, P], F32)
-            nc.scalar.copy(out=sum_sb[:, 0:blocks, :], in_=sum_t_of[i][:, 0:blocks, :])
-            rows = psum.tile([P, 2 * FEAT_BLOCKS, P], F32)
-            for c in range(blocks):
-                nc.tensor.transpose(rows[:, c, :], sum_sb[:, c, :], ident_f32[:])
-            rows_of[i] = rows
-
-        def by_pack(rows_half):
-            return rows_half.rearrange("n c q -> n (c q)").rearrange("n (p t) -> n t p", t=PACK)
-
-        def place_from_rows(i):
-            nc.scalar.copy(
-                out=hidden_of[i][:, :, 0:SRC_P], in_=by_pack(rows_of[i][:, 0:FEAT_BLOCKS, :])
-            )
-            if on_tensor(i):
-                nc.scalar.activation(
-                    out=hidden_of[i][:, :, SRC_P:P],
-                    in_=by_pack(rows_of[i][:, FEAT_BLOCKS : 2 * FEAT_BLOCKS, :]),
-                    func=ACT.Copy,
-                    scale=inv_count_of[i][:, 0:1],
-                )
-
-        def transpose_hidden(i):
             hidden_t = psum.tile([P, PACK, P], BF16)
             for t in range(PACK):
-                nc.tensor.transpose(hidden_t[:, t, :], hidden_of[i][:, t, :], ident[:])
-            return hidden_t
+                nc.tensor.transpose(hidden_t[:, t, :], hidden[:, t, :], ident[:])
+            hidden_ps_of[i] = hidden_t
 
-        def group_hidden(i, hidden_t):
+        def group_only(i):
             grouped = work.tile([P, P, PACK], BF16, align_bytes=64)
-            nc.scalar.copy(out=grouped[:], in_=hidden_t[:].rearrange("p t n -> p n t"))
+            nc.scalar.copy(out=grouped[:], in_=hidden_ps_of[i][:].rearrange("p t n -> p n t"))
             grouped_of[i] = grouped
 
         def quantise(i):
@@ -352,37 +361,58 @@ def tile_syntacticgcn_kernel(
                 )
                 nc.sync.dma_start(out=out[i * P : (i + 1) * P, cols], in_=result[:, cols])
 
-        def live(i):
-            return 0 <= i < NODE_TILES
+        def vector_tile_sums(i):
+            add_slot_quarters(i, 1)
+            add_slot_quarters(i, 0)
+            finish_slot_sums(i)
 
-        for step in range(NODE_TILES + 3):
-            if live(step):
-                if on_tensor(step):
-                    or_row_halves(step)
-                else:
-                    add_slot_halves(step)
-                test_rows_scalar(step)
-            if live(step - 3):
-                quantise(step - 3)
-                multiply(step - 3)
-            if live(step):
-                if on_tensor(step):
-                    finish_row_or(step)
-                else:
-                    finish_slot_sum(step)
-            if live(step - 1):
-                invert_count(step - 1)
-                new_hidden(step - 1)
-                if not on_tensor(step - 1):
-                    place_neigh_mean_from_tree(step - 1)
-            if live(step - 2):
-                place_from_rows(step - 2)
-                hidden_t = transpose_hidden(step - 2)
-            if live(step):
-                sum_on_tensor(step)
-            if live(step - 1):
-                sums_to_rows(step - 1)
-            if live(step - 2):
-                group_hidden(step - 2, hidden_t)
-            if live(step - 3):
-                finish(step - 3)
+        def tensor_tile_round(i):
+            invert_count(i)
+            if i + 1 < NODE_TILES:
+                sum_on_tensor(i + 1, 0)
+            spread_factor(i)
+            if i + 1 < NODE_TILES:
+                sum_on_tensor(i + 1, 1)
+            scale_and_group(i)
+            quantise(i)
+            multiply(i)
+
+        first_tensor_tile = len(VECTOR_TILES)
+        late_vector_tile = VECTOR_TILES[-1]
+        with tc.manual_schedule(engines={mybir.EngineType.PE, mybir.EngineType.Activation}):
+            test_rows_scalar(0, 0, SLOTS)
+            vector_tile_sums(0)
+            invert_count(0)
+            rows_to_hidden_ps(0)
+            test_rows_scalar(1, 0, SLOTS)
+            invert_count(1)
+            test_rows_scalar(2, 0, GROUP_COPY_AFTER)
+            group_only(0)
+            test_rows_scalar(2, GROUP_COPY_AFTER, SLOTS)
+            sum_on_tensor(2, 0)
+            sum_on_tensor(2, 1)
+            quantise(0)
+            multiply(0)
+            multiplied = [0]
+            finished = 0
+            for i in range(first_tensor_tile, NODE_TILES):
+                if i == LATE_TILE_ROUND:
+                    vector_tile_sums(late_vector_tile)
+                    rows_to_hidden_ps(late_vector_tile)
+                if i + 1 < NODE_TILES:
+                    test_rows_scalar(i + 1, 0, GROUP_COPY_AFTER)
+                    or_row_halves(i + 1)
+                    finish_row_or(i + 1)
+                    if i == LATE_TILE_ROUND:
+                        group_only(late_vector_tile)
+                    test_rows_scalar(i + 1, GROUP_COPY_AFTER, SLOTS)
+                tensor_tile_round(i)
+                multiplied.append(i)
+                finish(multiplied[finished])
+                finished += 1
+                if i == LATE_TILE_ROUND:
+                    quantise(late_vector_tile)
+                    multiply(late_vector_tile)
+                    multiplied.append(late_vector_tile)
+            for i in multiplied[finished:]:
+                finish(i)

@@ -21,6 +21,7 @@ FEAT = 256
 K = 2 * FEAT
 H = 1024
 N_TILE = 512
+H_BLOCKS = H // P
 GROUP = P // SLOTS
 GROUPS = P // GROUP
 SRC_P = FEAT // PACK
@@ -104,19 +105,36 @@ def tile_syntacticgcn_kernel(
 
         w_words = const.tile([P, PACK * H], U8, align_bytes=64)
         bias_all = const.tile([P, H], BF16)
+        bias_rows = const.tile([P, P], BF16)
+        nc.gpsimd.memset(bias_rows[:], 0.0)
 
-        def load_weights():
+        def load_small():
+            nc.sync.dma_start(out=bias_rows[0:H_BLOCKS, :], in_=b_map.rearrange("(c h) -> c h", c=H_BLOCKS))
             for quadrant in range(4):
                 nc.sync.dma_start(
                     out=w_scales[32 * quadrant : 32 * quadrant + 4, :].bitcast(I32),
                     in_=W_map_scales[0, 4 * quadrant : 4 * quadrant + 4, :].bitcast(I32),
                 )
+
+        def load_weights():
             nc.sync.dma_start(
                 out=w_words[:].bitcast(I32),
                 in_=W_map_words[0].rearrange("p n t -> p (n t)").bitcast(I32),
             )
-            nc.sync.dma_start(out=bias_all[:], in_=b_map.partition_broadcast(P))
 
+        def spread_bias():
+            bias_cols_ps = psum.tile([P, P], BF16, name="hidden_t")
+            nc.tensor.transpose(bias_cols_ps[:], bias_rows[:], ident[:])
+            bias_cols = const.tile([P, H_BLOCKS], BF16)
+            nc.vector.tensor_copy(out=bias_cols[:], in_=bias_cols_ps[:, 0:H_BLOCKS])
+            bias_ps = psum.tile([P, H], BF16, name="acc", bufs=3)
+            for c in range(H_BLOCKS):
+                nc.tensor.transpose(
+                    bias_ps[:, c * P : (c + 1) * P], bias_cols[:, c : c + 1].to_broadcast([P, P]), ident[:]
+                )
+            nc.vector.tensor_copy(out=bias_all[:], in_=bias_ps[:])
+
+        load_small()
         load(0)
         load(1)
         load(2)
@@ -379,6 +397,7 @@ def tile_syntacticgcn_kernel(
 
         first_tensor_tile = len(VECTOR_TILES)
         late_vector_tile = VECTOR_TILES[-1]
+        spread_bias()
         with tc.manual_schedule(engines={mybir.EngineType.PE, mybir.EngineType.Activation}):
             test_rows_scalar(0, 0, SLOTS)
             vector_tile_sums(0)

@@ -32,7 +32,7 @@ MAGNITUDE_BITS = 0x7FFF7FFF
 OR_STOP = 8
 
 VECTOR_TILES = (0, 1)
-SCALAR_ROWS = (16, 16, 16, 16, 16, 8, 8, 8)
+SCALAR_ROWS = (16, 16, 16, 16, 16, 16, 16, 16)
 
 GROUP_COPY_AFTER = 12
 LATE_TILE_ROUND = 3
@@ -122,12 +122,15 @@ def tile_syntacticgcn_kernel(
                 in_=W_map_words[0].rearrange("p n t -> p (n t)").bitcast(I32),
             )
 
-        def spread_bias():
+        bias_cols = const.tile([P, H_BLOCKS], BF16)
+
+        def bias_to_columns():
             bias_cols_ps = psum.tile([P, P], BF16, name="hidden_t")
             nc.tensor.transpose(bias_cols_ps[:], bias_rows[:], ident[:])
-            bias_cols = const.tile([P, H_BLOCKS], BF16)
             nc.vector.tensor_copy(out=bias_cols[:], in_=bias_cols_ps[:, 0:H_BLOCKS])
-            bias_ps = psum.tile([P, H], BF16, name="acc", bufs=3)
+
+        def spread_bias():
+            bias_ps = psum.tile([P, H], BF16, name="acc", bufs=4)
             for c in range(H_BLOCKS):
                 nc.tensor.transpose(
                     bias_ps[:, c * P : (c + 1) * P], bias_cols[:, c : c + 1].to_broadcast([P, P]), ident[:]
@@ -147,6 +150,8 @@ def tile_syntacticgcn_kernel(
         row_abs_of = {}
         inv_count_of = {}
         factor_of = {}
+        small_ps_of = {}
+        result_of = {}
         hidden_ps_of = {}
         grouped_of = {}
         codes_of = {}
@@ -238,48 +243,51 @@ def tile_syntacticgcn_kernel(
                 out=row_abs_of[i][:, first:SLOTS], in_=ored[:, :, 0:OR_STOP], axis=AX.X, op=ALU.max
             )
 
-        def invert_count(i):
+        def invert_count_of_rows(i):
+            valid = work.tile([P, SLOTS], F32)
+            count = work.tile([P, 1], F32)
+            nc.scalar.activation(out=valid[:], in_=row_abs_of[i][:], func=ACT.Sign, accum_out=count[:])
             at_least_one = work.tile([P, 1], F32)
-            if on_vector(i):
-                valid = work.tile([P, SLOTS], F32)
-                count = work.tile([P, 1], F32)
-                nc.scalar.activation(out=valid[:], in_=row_abs_of[i][:], func=ACT.Sign, accum_out=count[:])
-                nc.vector.tensor_scalar_max(out=at_least_one[:], in0=count[:], scalar1=1.0)
-            else:
-                masked = work.tile([P, GROUPS, GROUP], BF16)
-                nc.vector.scalar_tensor_tensor(
-                    out=masked[:],
-                    in0=row_abs_of[i][:].rearrange("q (g o) -> q g o", o=1).to_broadcast([P, GROUPS, GROUP]),
-                    scalar=0.0,
-                    in1=slot_sum[:].rearrange("q (o n) -> q o n", o=1).to_broadcast([P, GROUPS, GROUP]),
-                    op0=ALU.is_gt,
-                    op1=ALU.mult,
-                )
-                count_ps = psum.tile([P, 1], F32)
-                nc.tensor.matmul(
-                    out=count_ps[:],
-                    lhsT=masked[:].rearrange("q g n -> q (g n)"),
-                    rhs=ones_col[:],
-                    start=True,
-                    stop=True,
-                )
-                nc.vector.tensor_scalar_max(out=at_least_one[:], in0=count_ps[:], scalar1=1.0)
-            if on_vector(i):
-                inv_count = const.tile([P, 1], F32, name="inv_count_kept%d" % i)
-            else:
-                inv_count = work.tile([P, 1], F32)
+            nc.vector.tensor_scalar_max(out=at_least_one[:], in0=count[:], scalar1=1.0)
+            inv_count = const.tile([P, 1], F32, name="inv_count_kept%d" % i)
             nc.vector.reciprocal(out=inv_count[:], in_=at_least_one[:])
             inv_count_of[i] = inv_count
 
-        def spread_factor(i):
-            factor_row = factor_rows[i % 2]
-            nc.vector.tensor_copy(
-                out=factor_row[:, SRC_P:P], in_=inv_count_of[i][:, 0:1].to_broadcast([P, P - SRC_P])
+        def count_on_tensor(i):
+            masked = work.tile([P, GROUPS, GROUP], BF16)
+            nc.vector.scalar_tensor_tensor(
+                out=masked[:],
+                in0=row_abs_of[i][:].rearrange("q (g o) -> q g o", o=1).to_broadcast([P, GROUPS, GROUP]),
+                scalar=0.0,
+                in1=slot_sum[:].rearrange("q (o n) -> q o n", o=1).to_broadcast([P, GROUPS, GROUP]),
+                op0=ALU.is_gt,
+                op1=ALU.mult,
             )
-            factor_ps = psum.tile([P, P], F32)
-            nc.tensor.transpose(factor_ps[:], factor_row[:], ident_f32[:])
+            small_ps = psum.tile([P, P + 1], F32)
+            nc.tensor.matmul(
+                out=small_ps[:, P : P + 1],
+                lhsT=masked[:].rearrange("q g n -> q (g n)"),
+                rhs=ones_col[:],
+                start=True,
+                stop=True,
+            )
+            small_ps_of[i] = small_ps
+
+        def factor_to_rows(i):
+            at_least_one = work.tile([P, 1], F32)
+            nc.vector.tensor_scalar_max(out=at_least_one[:], in0=small_ps_of[i][:, P : P + 1], scalar1=1.0)
+            inv_count = work.tile([P, 1], F32)
+            nc.vector.reciprocal(out=inv_count[:], in_=at_least_one[:])
+            nc.vector.tensor_copy(
+                out=factor_rows[i % 2][:, SRC_P:P], in_=inv_count[:, 0:1].to_broadcast([P, P - SRC_P])
+            )
+
+        def transpose_factor(i):
+            nc.tensor.transpose(small_ps_of[i][:, 0:P], factor_rows[i % 2][:], ident_f32[:])
+
+        def copy_factor(i):
             factor = work.tile([P, P], F32)
-            nc.vector.tensor_copy(out=factor[:], in_=factor_ps[:])
+            nc.vector.tensor_copy(out=factor[:], in_=small_ps_of[i][:, 0:P])
             factor_of[i] = factor
 
         def sum_on_tensor(i, half):
@@ -349,7 +357,7 @@ def tile_syntacticgcn_kernel(
             codes, scales = codes_of[i]
             banks = []
             for h in range(H // N_TILE):
-                acc = psum.tile([P, N_TILE], F32, bufs=3)
+                acc = psum.tile([P, N_TILE], F32, bufs=4)
                 nc.tensor.matmul_mx(
                     out=acc[:],
                     lhsT=codes[:].bitcast(FP8X4),
@@ -362,49 +370,67 @@ def tile_syntacticgcn_kernel(
                 banks.append(acc)
             acc_of[i] = banks
 
+        def add_bias(i, h):
+            if h == 0:
+                result = results.tile([P, H], F32)
+                result_of[i] = result
+            cols = slice(h * N_TILE, (h + 1) * N_TILE)
+            nc.vector.tensor_tensor(
+                out=result_of[i][:, cols], in0=acc_of[i][h][:], in1=bias_all[:, cols], op=ALU.add
+            )
+
+        def leaky_and_store(i, h):
+            cols = slice(h * N_TILE, (h + 1) * N_TILE)
+            result = result_of[i]
+            nc.vector.scalar_tensor_tensor(
+                out=result[:, cols],
+                in0=result[:, cols],
+                scalar=NEG_SLOPE,
+                in1=result[:, cols],
+                op0=ALU.mult,
+                op1=ALU.max,
+            )
+            nc.sync.dma_start(out=out[i * P : (i + 1) * P, cols], in_=result[:, cols])
+
         def finish(i):
-            result = results.tile([P, H], F32)
-            for h in range(H // N_TILE):
-                cols = slice(h * N_TILE, (h + 1) * N_TILE)
-                nc.vector.tensor_tensor(
-                    out=result[:, cols], in0=acc_of[i][h][:], in1=bias_all[:, cols], op=ALU.add
-                )
-                nc.vector.scalar_tensor_tensor(
-                    out=result[:, cols],
-                    in0=result[:, cols],
-                    scalar=NEG_SLOPE,
-                    in1=result[:, cols],
-                    op0=ALU.mult,
-                    op1=ALU.max,
-                )
-                nc.sync.dma_start(out=out[i * P : (i + 1) * P, cols], in_=result[:, cols])
+            add_bias(i, 0)
+            add_bias(i, 1)
+            leaky_and_store(i, 0)
+            leaky_and_store(i, 1)
 
-        def vector_tile_sums(i):
-            add_slot_quarters(i, 1)
-            add_slot_quarters(i, 0)
-            finish_slot_sums(i)
-
-        def tensor_tile_round(i):
-            invert_count(i)
+        def tensor_tile_round(i, before):
+            count_on_tensor(i)
+            add_bias(before, 0)
             if i + 1 < NODE_TILES:
                 sum_on_tensor(i + 1, 0)
-            spread_factor(i)
+            factor_to_rows(i)
+            transpose_factor(i)
+            add_bias(before, 1)
             if i + 1 < NODE_TILES:
                 sum_on_tensor(i + 1, 1)
+            copy_factor(i)
             scale_and_group(i)
+            leaky_and_store(before, 0)
             quantise(i)
             multiply(i)
+            leaky_and_store(before, 1)
 
         first_tensor_tile = len(VECTOR_TILES)
         late_vector_tile = VECTOR_TILES[-1]
-        spread_bias()
-        with tc.manual_schedule(engines={mybir.EngineType.PE, mybir.EngineType.Activation}):
+        with tc.manual_schedule():
             test_rows_scalar(0, 0, SLOTS)
-            vector_tile_sums(0)
-            invert_count(0)
+            add_slot_quarters(0, 1)
+            bias_to_columns()
+            add_slot_quarters(0, 0)
+            spread_bias()
+            finish_slot_sums(0)
+            invert_count_of_rows(0)
             rows_to_hidden_ps(0)
             test_rows_scalar(1, 0, SLOTS)
-            invert_count(1)
+            add_slot_quarters(1, 1)
+            add_slot_quarters(1, 0)
+            invert_count_of_rows(1)
+            finish_slot_sums(1)
             test_rows_scalar(2, 0, GROUP_COPY_AFTER)
             group_only(0)
             test_rows_scalar(2, GROUP_COPY_AFTER, SLOTS)
@@ -416,19 +442,18 @@ def tile_syntacticgcn_kernel(
             finished = 0
             for i in range(first_tensor_tile, NODE_TILES):
                 if i == LATE_TILE_ROUND:
-                    vector_tile_sums(late_vector_tile)
                     rows_to_hidden_ps(late_vector_tile)
                 if i + 1 < NODE_TILES:
                     test_rows_scalar(i + 1, 0, GROUP_COPY_AFTER)
-                    or_row_halves(i + 1)
-                    finish_row_or(i + 1)
                     if i == LATE_TILE_ROUND:
                         group_only(late_vector_tile)
                     test_rows_scalar(i + 1, GROUP_COPY_AFTER, SLOTS)
-                tensor_tile_round(i)
-                multiplied.append(i)
-                finish(multiplied[finished])
+                tensor_tile_round(i, multiplied[finished])
                 finished += 1
+                multiplied.append(i)
+                if len(multiplied) - finished > 1:
+                    finish(multiplied[finished])
+                    finished += 1
                 if i == LATE_TILE_ROUND:
                     quantise(late_vector_tile)
                     multiply(late_vector_tile)

@@ -398,21 +398,26 @@ def tile_syntacticgcn_kernel(
             leaky_and_store(i, 0)
             leaky_and_store(i, 1)
 
-        def tensor_tile_round(i, before):
+        def tensor_tile_round(i, before, quantised):
+            last = i == NODE_TILES - 1
+            sum_on_tensor(i, 0)
+            for j in quantised:
+                multiply(j)
             count_on_tensor(i)
             add_bias(before, 0)
-            if i + 1 < NODE_TILES:
-                sum_on_tensor(i + 1, 0)
+            sum_on_tensor(i, 1)
             factor_to_rows(i)
             transpose_factor(i)
             add_bias(before, 1)
-            if i + 1 < NODE_TILES:
-                sum_on_tensor(i + 1, 1)
             copy_factor(i)
             scale_and_group(i)
-            leaky_and_store(before, 0)
-            quantise(i)
-            multiply(i)
+            if last:
+                quantise(i)
+                multiply(i)
+                leaky_and_store(before, 0)
+            else:
+                leaky_and_store(before, 0)
+                quantise(i)
             leaky_and_store(before, 1)
 
         first_tensor_tile = len(VECTOR_TILES)
@@ -434,11 +439,9 @@ def tile_syntacticgcn_kernel(
             test_rows_scalar(2, 0, GROUP_COPY_AFTER)
             group_only(0)
             test_rows_scalar(2, GROUP_COPY_AFTER, SLOTS)
-            sum_on_tensor(2, 0)
-            sum_on_tensor(2, 1)
             quantise(0)
-            multiply(0)
-            multiplied = [0]
+            quantised = [0]
+            in_line = [0]
             finished = 0
             for i in range(first_tensor_tile, NODE_TILES):
                 if i == LATE_TILE_ROUND:
@@ -448,15 +451,16 @@ def tile_syntacticgcn_kernel(
                     if i == LATE_TILE_ROUND:
                         group_only(late_vector_tile)
                     test_rows_scalar(i + 1, GROUP_COPY_AFTER, SLOTS)
-                tensor_tile_round(i, multiplied[finished])
+                tensor_tile_round(i, in_line[finished], quantised)
                 finished += 1
-                multiplied.append(i)
-                if len(multiplied) - finished > 1:
-                    finish(multiplied[finished])
+                if len(in_line) - finished > 0:
+                    finish(in_line[finished])
                     finished += 1
+                quantised = [i]
+                in_line.append(i)
                 if i == LATE_TILE_ROUND:
                     quantise(late_vector_tile)
-                    multiply(late_vector_tile)
-                    multiplied.append(late_vector_tile)
-            for i in multiplied[finished:]:
+                    quantised.append(late_vector_tile)
+                    in_line.append(late_vector_tile)
+            for i in in_line[finished:]:
                 finish(i)

@@ -56,6 +56,8 @@ def tile_syntacticgcn_kernel(
 
         w_scales = const.tile([P, H], U8, align_bytes=64)
         nc.vector.memset(w_scales[:].bitcast(I32), 0)
+        bias_rows = const.tile([P, P], BF16)
+        nc.gpsimd.memset(bias_rows[:], 0.0)
         ident = const.tile([P, P], BF16)
         make_identity(nc, ident[:])
         ident_f32 = const.tile([P, P], F32)
@@ -105,8 +107,6 @@ def tile_syntacticgcn_kernel(
 
         w_words = const.tile([P, PACK * H], U8, align_bytes=64)
         bias_all = const.tile([P, H], BF16)
-        bias_rows = const.tile([P, P], BF16)
-        nc.gpsimd.memset(bias_rows[:], 0.0)
 
         def load_small():
             nc.sync.dma_start(out=bias_rows[0:H_BLOCKS, :], in_=b_map.rearrange("(c h) -> c h", c=H_BLOCKS))
@@ -137,8 +137,8 @@ def tile_syntacticgcn_kernel(
                 )
             nc.vector.tensor_copy(out=bias_all[:], in_=bias_ps[:])
 
-        load_small()
         load(0)
+        load_small()
         load(1)
         load(2)
         load_weights()

@@ -31,11 +31,69 @@ WORDS = FEAT // 2
 MAGNITUDE_BITS = 0x7FFF7FFF
 OR_STOP = 8
 
-VECTOR_TILES = (0, 1)
-SCALAR_ROWS = (16, 16, 16, 16, 16, 16, 16, 16)
+ROW_TILES = (0, 1,)
+GPSIMD_TILES = ()
+CHUNK = {0: 4, 1: 4}
+LOADS = "n0x4 s0 small n1 n2 s1 n3 s2 n4 w s3 n5 s4 n6 s5 n7 s6x2 s7x2"
+ORDER = """
 
-GROUP_COPY_AFTER = 12
-LATE_TILE_ROUND = 3
+tests:0,0,16
+trees:0
+bcols bspread
+inv:0 rows:0
+tests:1,0,16
+trees:1
+inv:1
+tests:2,0,12 group:0 tests:2,12,16
+tests:3,0,16
+ mask:2 cnt:2  fmax:2
+sum:2,0,8
+quant:0 mul:0 frecip:2  fspread:2 ft:2 
+sum:2,8,16
+
+add:0,0 fcopy:2 add:0,1
+
+
+rows:1 tests:4,0,8 group:1 tests:4,8,16
+ mask:3 cnt:3 scale:2 fmax:3
+sum:3,0,8
+quant:2 mul:2 frecip:3 leaky:0,0 fspread:3 ft:3 leaky:0,1
+sum:3,8,16
+
+add:2,0 fcopy:3 add:2,1
+
+
+tests:5,0,16
+ mask:4 cnt:4 scale:3 fmax:4
+sum:4,0,8
+quant:3 mul:3 frecip:4 leaky:2,0 fspread:4 ft:4 leaky:2,1
+sum:4,8,16
+
+add:3,0 fcopy:4 add:3,1
+quant:1
+
+tests:6,0,16
+mul:1 mask:5 cnt:5 scale:4 fmax:5
+sum:5,0,8
+quant:4 mul:4 frecip:5 leaky:3,0 fspread:5 ft:5 leaky:3,1
+sum:5,8,16
+add:1,0 add:1,1 leaky:1,0 leaky:1,1
+add:4,0 fcopy:5 add:4,1
+
+
+tests:7,0,16
+ mask:6 cnt:6 scale:5 fmax:6
+sum:6,0,8
+quant:5 mul:5 frecip:6 leaky:4,0 fspread:6 ft:6 leaky:4,1
+sum:6,8,16
+
+add:5,0 fcopy:6 add:5,1
+
+
+sum:7,0,8
+mask:7 cnt:7 scale:6 fmax:7 sum:7,8,16 quant:6 frecip:7 leaky:5,0 fspread:7 ft:7 leaky:5,1 mul:6 fcopy:7 scale:7 add:6,0 quant:7 mul:7 add:6,1 leaky:6,0 leaky:6,1 add:7,0 add:7,1 leaky:7,0 leaky:7,1
+
+"""
 
 FLOPS = 2 * NODE_TILES * P * K * H
 
@@ -51,8 +109,8 @@ def tile_syntacticgcn_kernel(
         results = ctx.enter_context(tc.tile_pool(name="results", bufs=NODE_TILES))
         psum = ctx.enter_context(tc.psum_pool(name="psum", bufs=1))
 
-        def on_vector(i):
-            return i in VECTOR_TILES
+        def on_rows(i):
+            return i in ROW_TILES
 
         w_scales = const.tile([P, H], U8, align_bytes=64)
         nc.vector.memset(w_scales[:].bitcast(I32), 0)
@@ -86,24 +144,25 @@ def tile_syntacticgcn_kernel(
         def by_slot(features):
             return features.rearrange("s m d -> (s m) d").rearrange("(g p) d -> p g d", p=P)
 
-        def load(i):
-            if on_vector(i):
-                neigh_tile = inputs.tile([P, SLOTS, FEAT], BF16, name="neigh%d" % i)
-                pieces = FIRST_LOAD_PIECES if i == 0 else 1
+        def load(kind, i, pieces=1):
+            features = (src_node_features if kind == "s" else neigh_node_features)[i]
+            if on_rows(i):
+                tiles = src_tiles if kind == "s" else neigh_tiles
+                tile = inputs.tile([P, SLOTS, FEAT], BF16, name="%s%d" % (kind, i))
                 step = SLOTS // pieces
                 for m in range(0, SLOTS, step):
-                    nc.sync.dma_start(
-                        out=neigh_tile[:, m : m + step, :], in_=neigh_node_features[i][:, m : m + step, :]
-                    )
-                neigh_tiles[i] = neigh_tile
-                src_tile = inputs.tile([P, SLOTS, FEAT], BF16, name="src%d" % i)
-                nc.sync.dma_start(out=src_tile[:], in_=src_node_features[i])
-                src_tiles[i] = src_tile
+                    nc.sync.dma_start(out=tile[:, m : m + step, :], in_=features[:, m : m + step, :])
+                tiles[i] = tile
             else:
-                both = inputs.tile([P, GROUPS, K], BF16, name="both%d" % i)
-                nc.sync.dma_start(out=both[:, :, FEAT:K], in_=by_slot(neigh_node_features[i]))
-                nc.sync.dma_start(out=both[:, :, 0:FEAT], in_=by_slot(src_node_features[i]))
-                both_tiles[i] = both
+                if i not in both_tiles:
+                    both = inputs.tile([P, GROUPS, K], BF16, name="both%d" % i)
+                    both_tiles[i] = both
+                cols = slice(0, FEAT) if kind == "s" else slice(FEAT, K)
+                step = GROUPS // pieces
+                for g in range(0, GROUPS, step):
+                    nc.sync.dma_start(
+                        out=both_tiles[i][:, g : g + step, cols], in_=by_slot(features)[:, g : g + step, :]
+                    )
 
         w_words = const.tile([P, PACK * H], U8, align_bytes=64)
         bias_all = const.tile([P, H], BF16)
@@ -137,15 +196,17 @@ def tile_syntacticgcn_kernel(
                 )
             nc.vector.tensor_copy(out=bias_all[:], in_=bias_ps[:])
 
-        load(0)
-        load_small()
-        load(1)
-        load(2)
-        load_weights()
-        for i in range(3, NODE_TILES):
-            load(i)
+        for item in LOADS.split():
+            if item == "small":
+                load_small()
+            elif item == "w":
+                load_weights()
+            else:
+                load(item[0], int(item[1]), int(item[3]) if len(item) > 2 else 1)
 
         partial_of = {}
+        masked_of = {}
+        alo_of = {}
         or_of = {}
         row_abs_of = {}
         inv_count_of = {}
@@ -158,90 +219,64 @@ def tile_syntacticgcn_kernel(
         acc_of = {}
 
         def neigh_row(i, r):
-            if on_vector(i):
+            if on_rows(i):
                 return neigh_tiles[i][:, r, :]
             return both_tiles[i][:, r, FEAT:K]
 
-        def add_slot_quarters(i, which):
+        def engine_of(i):
+            return nc.gpsimd if i in GPSIMD_TILES else nc.vector
+
+        def add_quarter(i, which, q):
             tile = (src_tiles if which == 0 else neigh_tiles)[i]
-            partial = work.tile([P, SLOTS // 2, FEAT], F32, name="partial%d" % which)
             quarter = SLOTS // 4
-            for half in range(2):
-                first = 2 * half * quarter
-                nc.vector.tensor_tensor(
-                    out=partial[:, half * quarter : (half + 1) * quarter, :],
-                    in0=tile[:, first : first + quarter, :],
-                    in1=tile[:, first + quarter : first + 2 * quarter, :],
+            if q == 1:
+                tag = "partial%d%s" % (which, "g" if i in GPSIMD_TILES else "v")
+                partial = work.tile([P, quarter, FEAT], F32, name=tag)
+                partial_of[(i, which)] = partial
+            partial = partial_of[(i, which)]
+            for m in range(0, quarter, CHUNK[i]):
+                engine_of(i).tensor_tensor(
+                    out=partial[:, m : m + CHUNK[i], :],
+                    in0=tile[:, q * quarter + m : q * quarter + m + CHUNK[i], :],
+                    in1=tile[:, m : m + CHUNK[i], :] if q == 1 else partial[:, m : m + CHUNK[i], :],
                     op=ALU.add,
                 )
-            partial_of[(i, which)] = partial
 
-        def finish_slot_sums(i):
-            width = SLOTS // 2
-            while width > 1:
-                width //= 2
-                for which in (1, 0):
-                    partial = partial_of[(i, which)]
-                    nc.vector.tensor_tensor(
-                        out=partial[:, 0:width, :],
-                        in0=partial[:, 0:width, :],
-                        in1=partial[:, width : 2 * width, :],
-                        op=ALU.add,
-                    )
+        def fold(i, which, width):
+            partial = partial_of[(i, which)]
+            engine_of(i).tensor_tensor(
+                out=partial[:, 0:width, :],
+                in0=partial[:, 0:width, :],
+                in1=partial[:, width : 2 * width, :],
+                op=ALU.add,
+            )
+
+        def tree(i, which):
+            for q in (1, 2, 3):
+                add_quarter(i, which, q)
+            fold(i, which, 2)
+            fold(i, which, 1)
+
+        def two_trees(i):
+            for q in (1, 2, 3):
+                add_quarter(i, 1, q)
+            add_quarter(i, 0, 1)
+            fold(i, 1, 2)
+            add_quarter(i, 0, 2)
+            fold(i, 1, 1)
+            add_quarter(i, 0, 3)
+            fold(i, 0, 2)
+            fold(i, 0, 1)
 
         def test_rows_scalar(i, first, last):
             if first == 0:
-                row_abs = work.tile([P, SLOTS], F32, bufs=3)
+                row_abs = work.tile([P, SLOTS], F32, bufs=NODE_TILES)
                 row_abs_of[i] = row_abs
-            for r in range(first, min(last, SCALAR_ROWS[i])):
+            for r in range(first, last):
                 unused = work.tile([P, FEAT], BF16)
                 nc.scalar.activation(
                     out=unused[:], in_=neigh_row(i, r), func=ACT.Abs, accum_out=row_abs_of[i][:, r : r + 1]
                 )
-
-        def or_row_halves(i):
-            first = SCALAR_ROWS[i]
-            if first == SLOTS:
-                return
-            if on_vector(i):
-                words = neigh_tiles[i][:].rearrange("p r f -> p (r f)").bitcast(I32)
-                words = words.rearrange("p (r w) -> p r w", w=WORDS)
-            else:
-                words = both_tiles[i][:].rearrange("p r f -> p (r f)").bitcast(I32)
-                words = words.rearrange("p (r w) -> p r w", w=2 * WORDS)[:, :, WORDS : 2 * WORDS]
-            ored = work.tile([P, SLOTS - first, WORDS // 2], I32)
-            nc.vector.tensor_tensor(
-                out=ored[:],
-                in0=words[:, first:SLOTS, 0 : WORDS // 2],
-                in1=words[:, first:SLOTS, WORDS // 2 : WORDS],
-                op=ALU.bitwise_or,
-            )
-            or_of[i] = ored
-
-        def finish_row_or(i):
-            first = SCALAR_ROWS[i]
-            if first == SLOTS:
-                return
-            ored = or_of[i]
-            width = WORDS // 2
-            while width > OR_STOP:
-                width //= 2
-                nc.vector.tensor_tensor(
-                    out=ored[:, :, 0:width],
-                    in0=ored[:, :, 0:width],
-                    in1=ored[:, :, width : 2 * width],
-                    op=ALU.bitwise_or,
-                )
-            nc.vector.tensor_scalar(
-                out=ored[:, :, 0:OR_STOP],
-                in0=ored[:, :, 0:OR_STOP],
-                scalar1=MAGNITUDE_BITS,
-                scalar2=None,
-                op0=ALU.bitwise_and,
-            )
-            nc.vector.tensor_reduce(
-                out=row_abs_of[i][:, first:SLOTS], in_=ored[:, :, 0:OR_STOP], axis=AX.X, op=ALU.max
-            )
 
         def invert_count_of_rows(i):
             valid = work.tile([P, SLOTS], F32)
@@ -263,6 +298,10 @@ def tile_syntacticgcn_kernel(
                 op0=ALU.is_gt,
                 op1=ALU.mult,
             )
+            masked_of[i] = masked
+
+        def count_matmul(i):
+            masked = masked_of[i]
             small_ps = psum.tile([P, P + 1], F32)
             nc.tensor.matmul(
                 out=small_ps[:, P : P + 1],
@@ -276,8 +315,15 @@ def tile_syntacticgcn_kernel(
         def factor_to_rows(i):
             at_least_one = work.tile([P, 1], F32)
             nc.vector.tensor_scalar_max(out=at_least_one[:], in0=small_ps_of[i][:, P : P + 1], scalar1=1.0)
+            alo_of[i] = at_least_one
+
+        def frecip(i):
             inv_count = work.tile([P, 1], F32)
-            nc.vector.reciprocal(out=inv_count[:], in_=at_least_one[:])
+            nc.vector.reciprocal(out=inv_count[:], in_=alo_of[i][:])
+            inv_count_of[i] = inv_count
+
+        def fspread(i):
+            inv_count = inv_count_of[i]
             nc.vector.tensor_copy(
                 out=factor_rows[i % 2][:, SRC_P:P], in_=inv_count[:, 0:1].to_broadcast([P, P - SRC_P])
             )
@@ -290,13 +336,13 @@ def tile_syntacticgcn_kernel(
             nc.vector.tensor_copy(out=factor[:], in_=small_ps_of[i][:, 0:P])
             factor_of[i] = factor
 
-        def sum_on_tensor(i, half):
-            if half == 0:
+        def sum_on_tensor(i, first, last):
+            if first == 0:
                 hidden_ps = psum.tile([P, PACK, P], F32, bufs=2)
                 hidden_ps_of[i] = hidden_ps
             hidden_ps = hidden_ps_of[i]
-            for t in range(half * PACK // 2, (half + 1) * PACK // 2):
-                for g in range(GROUPS):
+            for g in range(first, last):
+                for t in range(PACK):
                     nc.tensor.matmul(
                         out=hidden_ps[:, t, g * GROUP : (g + 1) * GROUP],
                         lhsT=both_tiles[i][:, g, t:K:PACK],
@@ -398,69 +444,32 @@ def tile_syntacticgcn_kernel(
             leaky_and_store(i, 0)
             leaky_and_store(i, 1)
 
-        def tensor_tile_round(i, before, quantised):
-            last = i == NODE_TILES - 1
-            sum_on_tensor(i, 0)
-            for j in quantised:
-                multiply(j)
-            count_on_tensor(i)
-            add_bias(before, 0)
-            sum_on_tensor(i, 1)
-            factor_to_rows(i)
-            transpose_factor(i)
-            add_bias(before, 1)
-            copy_factor(i)
-            scale_and_group(i)
-            if last:
-                quantise(i)
-                multiply(i)
-                leaky_and_store(before, 0)
-            else:
-                leaky_and_store(before, 0)
-                quantise(i)
-            leaky_and_store(before, 1)
-
-        first_tensor_tile = len(VECTOR_TILES)
-        late_vector_tile = VECTOR_TILES[-1]
+        verbs = {
+            "tests": test_rows_scalar,
+            "trees": two_trees,
+            "quarter": add_quarter,
+            "fold": fold,
+            "tree": tree,
+            "inv": invert_count_of_rows,
+            "rows": rows_to_hidden_ps,
+            "group": group_only,
+            "quant": quantise,
+            "mul": multiply,
+            "mask": count_on_tensor,
+            "cnt": count_matmul,
+            "fmax": factor_to_rows,
+            "frecip": frecip,
+            "fspread": fspread,
+            "ft": transpose_factor,
+            "fcopy": copy_factor,
+            "sum": sum_on_tensor,
+            "scale": scale_and_group,
+            "add": add_bias,
+            "leaky": leaky_and_store,
+            "bcols": bias_to_columns,
+            "bspread": spread_bias,
+        }
         with tc.manual_schedule():
-            test_rows_scalar(0, 0, SLOTS)
-            add_slot_quarters(0, 1)
-            bias_to_columns()
-            add_slot_quarters(0, 0)
-            spread_bias()
-            finish_slot_sums(0)
-            invert_count_of_rows(0)
-            rows_to_hidden_ps(0)
-            test_rows_scalar(1, 0, SLOTS)
-            add_slot_quarters(1, 1)
-            add_slot_quarters(1, 0)
-            invert_count_of_rows(1)
-            finish_slot_sums(1)
-            test_rows_scalar(2, 0, GROUP_COPY_AFTER)
-            group_only(0)
-            test_rows_scalar(2, GROUP_COPY_AFTER, SLOTS)
-            quantise(0)
-            quantised = [0]
-            in_line = [0]
-            finished = 0
-            for i in range(first_tensor_tile, NODE_TILES):
-                if i == LATE_TILE_ROUND:
-                    rows_to_hidden_ps(late_vector_tile)
-                if i + 1 < NODE_TILES:
-                    test_rows_scalar(i + 1, 0, GROUP_COPY_AFTER)
-                    if i == LATE_TILE_ROUND:
-                        group_only(late_vector_tile)
-                    test_rows_scalar(i + 1, GROUP_COPY_AFTER, SLOTS)
-                tensor_tile_round(i, in_line[finished], quantised)
-                finished += 1
-                if len(in_line) - finished > 0:
-                    finish(in_line[finished])
-                    finished += 1
-                quantised = [i]
-                in_line.append(i)
-                if i == LATE_TILE_ROUND:
-                    quantise(late_vector_tile)
-                    quantised.append(late_vector_tile)
-                    in_line.append(late_vector_tile)
-            for i in in_line[finished:]:
-                finish(i)
+            for word in ORDER.split():
+                parts = word.split(":")
+                verbs[parts[0]](*[int(x) for part in parts[1:] for x in part.split(",")])

@@ -32,9 +32,9 @@ MAGNITUDE_BITS = 0x7FFF7FFF
 OR_STOP = 8
 
 ROW_TILES = (0, 1,)
-GPSIMD_TILES = ()
-CHUNK = {0: 4, 1: 4}
-LOADS = "n0x4 s0 small n1 n2 s1 n3 s2 n4 w s3 n5 s4 n6 s5 n7 s6x2 s7x2"
+GPSIMD_TREES = ()
+CHUNK = 2
+LOADS = "n0x4 s0 small n1 n2 s1 n3 s2 n4x2 w s3x2 n5x2 s4x2 n6x2 s5x4 n7x2 s6x4 s7x4"
 ORDER = """
 
 tests:0,0,16
@@ -77,21 +77,18 @@ mul:1 mask:5 cnt:5 scale:4 fmax:5
 sum:5,0,8
 quant:4 mul:4 frecip:5 leaky:3,0 fspread:5 ft:5 leaky:3,1
 sum:5,8,16
-add:1,0 add:1,1 leaky:1,0 leaky:1,1
+add:1,0 add:1,1
 add:4,0 fcopy:5 add:4,1
 
 
 tests:7,0,16
- mask:6 cnt:6 scale:5 fmax:6
-sum:6,0,8
-quant:5 mul:5 frecip:6 leaky:4,0 fspread:6 ft:6 leaky:4,1
-sum:6,8,16
-
+ mask:6 cnt:6 scale:5 fmax:6 quant:5 mul:5
+sum:6,0,4 
+frecip:6 leaky:4,0 fspread:6 ft:6 leaky:4,1
+sum:6,4,8 sum:6,8,12 sum:6,12,16 
 add:5,0 fcopy:6 add:5,1
-
-
-sum:7,0,8
-mask:7 cnt:7 scale:6 fmax:7 sum:7,8,16 quant:6 frecip:7 leaky:5,0 fspread:7 ft:7 leaky:5,1 mul:6 fcopy:7 scale:7 add:6,0 quant:7 mul:7 add:6,1 leaky:6,0 leaky:6,1 add:7,0 add:7,1 leaky:7,0 leaky:7,1
+leaky:1,0 mask:7 cnt:7 leaky:1,1 fmax:7 scale:6 frecip:7 sum:7,0,4 sum:7,4,8  quant:6 fspread:7 leaky:5,0 leaky:5,1 mul:6,0,1 ft:7 sum:7,8,12 sum:7,12,16  mul:6,1,2
+fcopy:7 add:6,0 leaky:6,0 scale:7 add:6,1 quant:7 mul:7 leaky:6,1 add:7,0 add:7,1 leaky:7,0 leaky:7,1
 
 """
 
@@ -144,7 +141,7 @@ def tile_syntacticgcn_kernel(
         def by_slot(features):
             return features.rearrange("s m d -> (s m) d").rearrange("(g p) d -> p g d", p=P)
 
-        def load(kind, i, pieces=1):
+        def load(kind, i, pieces=1, queue=nc.sync):
             features = (src_node_features if kind == "s" else neigh_node_features)[i]
             if on_rows(i):
                 tiles = src_tiles if kind == "s" else neigh_tiles
@@ -160,7 +157,7 @@ def tile_syntacticgcn_kernel(
                 cols = slice(0, FEAT) if kind == "s" else slice(FEAT, K)
                 step = GROUPS // pieces
                 for g in range(0, GROUPS, step):
-                    nc.sync.dma_start(
+                    queue.dma_start(
                         out=both_tiles[i][:, g : g + step, cols], in_=by_slot(features)[:, g : g + step, :]
                     )
 
@@ -202,7 +199,12 @@ def tile_syntacticgcn_kernel(
             elif item == "w":
                 load_weights()
             else:
-                load(item[0], int(item[1]), int(item[3]) if len(item) > 2 else 1)
+                load(
+                    item[0],
+                    int(item[1]),
+                    int(item[3]) if len(item) > 2 else 1,
+                    nc.scalar if item[len(item) - 1] == "A" else nc.sync,
+                )
 
         partial_of = {}
         masked_of = {}
@@ -223,28 +225,31 @@ def tile_syntacticgcn_kernel(
                 return neigh_tiles[i][:, r, :]
             return both_tiles[i][:, r, FEAT:K]
 
-        def engine_of(i):
-            return nc.gpsimd if i in GPSIMD_TILES else nc.vector
+        def engine_of(i, which):
+            return nc.gpsimd if (i, which) in GPSIMD_TREES else nc.vector
+
+        def chunk_of(i, which):
+            return CHUNK if (i, which) in GPSIMD_TREES else SLOTS // 4
 
         def add_quarter(i, which, q):
             tile = (src_tiles if which == 0 else neigh_tiles)[i]
             quarter = SLOTS // 4
             if q == 1:
-                tag = "partial%d%s" % (which, "g" if i in GPSIMD_TILES else "v")
+                tag = "partial%d%s" % (which, "g" if (i, which) in GPSIMD_TREES else "v")
                 partial = work.tile([P, quarter, FEAT], F32, name=tag)
                 partial_of[(i, which)] = partial
             partial = partial_of[(i, which)]
-            for m in range(0, quarter, CHUNK[i]):
-                engine_of(i).tensor_tensor(
-                    out=partial[:, m : m + CHUNK[i], :],
-                    in0=tile[:, q * quarter + m : q * quarter + m + CHUNK[i], :],
-                    in1=tile[:, m : m + CHUNK[i], :] if q == 1 else partial[:, m : m + CHUNK[i], :],
+            for m in range(0, quarter, chunk_of(i, which)):
+                engine_of(i, which).tensor_tensor(
+                    out=partial[:, m : m + chunk_of(i, which), :],
+                    in0=tile[:, q * quarter + m : q * quarter + m + chunk_of(i, which), :],
+                    in1=tile[:, m : m + chunk_of(i, which), :] if q == 1 else partial[:, m : m + chunk_of(i, which), :],
                     op=ALU.add,
                 )
 
         def fold(i, which, width):
             partial = partial_of[(i, which)]
-            engine_of(i).tensor_tensor(
+            engine_of(i, which).tensor_tensor(
                 out=partial[:, 0:width, :],
                 in0=partial[:, 0:width, :],
                 in1=partial[:, width : 2 * width, :],
@@ -399,10 +404,12 @@ def tile_syntacticgcn_kernel(
             )
             codes_of[i] = (codes, scales)
 
-        def multiply(i):
+        def multiply(i, first=0, last=2):
             codes, scales = codes_of[i]
-            banks = []
-            for h in range(H // N_TILE):
+            if first == 0:
+                acc_of[i] = []
+            banks = acc_of[i]
+            for h in range(first, last):
                 acc = psum.tile([P, N_TILE], F32, bufs=4)
                 nc.tensor.matmul_mx(
                     out=acc[:],
@@ -414,7 +421,6 @@ def tile_syntacticgcn_kernel(
                     stop=True,
                 )
                 banks.append(acc)
-            acc_of[i] = banks
 
         def add_bias(i, h):
             if h == 0:
@@ -446,6 +452,8 @@ def tile_syntacticgcn_kernel(
 
         verbs = {
             "tests": test_rows_scalar,
+            "ssrc": lambda i, pieces: load("s", i, pieces, nc.scalar),
+            "gsrc": lambda i, pieces: load("s", i, pieces, nc.gpsimd),
             "trees": two_trees,
             "quarter": add_quarter,
             "fold": fold,

@@ -31,64 +31,32 @@ WORDS = FEAT // 2
 MAGNITUDE_BITS = 0x7FFF7FFF
 OR_STOP = 8
 
-ROW_TILES = (0, 1,)
+ROW_TILES = (0, 1, 2,)
 GPSIMD_TREES = ()
+HALF_TREES = ((0, 1),)
 CHUNK = 2
-LOADS = "n0x4 s0 small n1 n2 s1 n3 s2 n4x2 w s3x2 n5x2 s4x2 n6x2 s5x4 n7x2 s6x4 s7x4"
+LOADS = "n0x4 s0 small n1 s1 n2 s2 n3 s3 w n4 s4x2 n5 n6 s5x4 n7x2 s6x4 s7x4"
 ORDER = """
 
-tests:0,0,16
-trees:0
-bcols bspread
-inv:0 rows:0
-tests:1,0,16
-trees:1
-inv:1
-tests:2,0,12 group:0 tests:2,12,16
-tests:3,0,16
- mask:2 cnt:2  fmax:2
-sum:2,0,8
-quant:0 mul:0 frecip:2  fspread:2 ft:2 
-sum:2,8,16
-
-add:0,0 fcopy:2 add:0,1
-
-
-rows:1 tests:4,0,8 group:1 tests:4,8,16
- mask:3 cnt:3 scale:2 fmax:3
-sum:3,0,8
-quant:2 mul:2 frecip:3 leaky:0,0 fspread:3 ft:3 leaky:0,1
-sum:3,8,16
-
-add:2,0 fcopy:3 add:2,1
-
-
-tests:5,0,16
- mask:4 cnt:4 scale:3 fmax:4
+tests:0,0,16 sgn:0
+quarter:0,1,1 quarter:0,1,2 quarter:0,1,3 quarter:0,0,1 fold:0,1,2 quarter:0,0,2 fold:0,1,1 quarter:0,0,3 bcols bspread fold:0,0,2
+tests:1,0,16 sgn:1
+quarter:1,1,1 fold:0,0,1 quarter:1,0,1 imax:0 quarter:1,1,2 irec:0 rows:0 quarter:1,0,2 quarter:1,1,3 quarter:1,0,3 fold:1,1,2 fold:1,0,2 bcopy fold:1,1,1 fold:1,0,1
+tests:2,0,16 sgn:2
+tests:3,0,5 group:0 tests:3,5,16
+quarter:2,1,1 imax:1 quarter:2,0,1 irec:1 sum:3,0,16 quarter:2,1,2 quarter:2,0,2 quant:0 mul:0 rows:1 quarter:2,1,3 mask:3 cnt:3 quarter:2,0,3 fmax:3 fold:2,1,2 frecip:3 imax:2 fold:2,0,2 irec:2 fspread:3 ft:3 fold:2,1,1 fold:2,0,1 fcopy:3
 sum:4,0,8
-quant:3 mul:3 frecip:4 leaky:2,0 fspread:4 ft:4 leaky:2,1
-sum:4,8,16
-
-add:3,0 fcopy:4 add:3,1
-quant:1
-
+tests:4,0,9 group:1 tests:4,9,16
+tests:5,0,4
+scale:3 add:0,0 quant:3 rows:2 mul:3 group:2 tests:5,4,16
+add:0,1 quant:1 leaky:0,0 mask:4 cnt:4 mul:1 sum:4,8,16 leaky:0,1 
 tests:6,0,16
-mul:1 mask:5 cnt:5 scale:4 fmax:5
-sum:5,0,8
-quant:4 mul:4 frecip:5 leaky:3,0 fspread:5 ft:5 leaky:3,1
-sum:5,8,16
-add:1,0 add:1,1
-add:4,0 fcopy:5 add:4,1
-
-
+add:3,0 fmax:4 add:3,1 frecip:4 leaky:3,0 fspread:4 ft:4 quant:2 mul:2 leaky:3,1 fcopy:4 add:1,0 scale:4 add:1,1 quant:4 sum:5,0,4 sum:5,4,8  mul:4 leaky:1,0 leaky:1,1
+mask:5 cnt:5 sum:5,8,12 sum:5,12,16 
 tests:7,0,16
- mask:6 cnt:6 scale:5 fmax:6 quant:5 mul:5
-sum:6,0,4 
-frecip:6 leaky:4,0 fspread:6 ft:6 leaky:4,1
-sum:6,4,8 sum:6,8,12 sum:6,12,16 
-add:5,0 fcopy:6 add:5,1
-leaky:1,0 mask:7 cnt:7 leaky:1,1 fmax:7 scale:6 frecip:7 sum:7,0,4 sum:7,4,8  quant:6 fspread:7 leaky:5,0 leaky:5,1 mul:6,0,1 ft:7 sum:7,8,12 sum:7,12,16  mul:6,1,2
-fcopy:7 add:6,0 leaky:6,0 scale:7 add:6,1 quant:7 mul:7 leaky:6,1 add:7,0 add:7,1 leaky:7,0 leaky:7,1
+
+add:4,0 fmax:5 add:4,1 frecip:5 leaky:4,0 fspread:5 ft:5 leaky:4,1 fcopy:5 sum:6,0,4  add:2,0 scale:5 mask:6 cnt:6 quant:5 add:2,1 fmax:6 sum:6,4,8 sum:6,8,12  leaky:2,0 frecip:6 mul:5 leaky:2,1 fspread:6 ft:6 sum:6,12,16  add:5,0 fcopy:6 add:5,1 sum:7,0,4 sum:7,4,8  leaky:5,0 scale:6
+mask:7 cnt:7 quant:6 mul:6,0,1 leaky:5,1 fmax:7 frecip:7 sum:7,8,12  fspread:7 ft:7 sum:7,12,16  mul:6,1,2 add:6,0 fcopy:7 leaky:6,0 scale:7 add:6,1 quant:7 mul:7 leaky:6,1 add:7,0 add:7,1 leaky:7,0 leaky:7,1
 
 """
 
@@ -180,6 +148,8 @@ def tile_syntacticgcn_kernel(
 
         bias_cols = const.tile([P, H_BLOCKS], BF16)
 
+        bspread_ps = {}
+
         def bias_to_columns():
             bias_cols_ps = psum.tile([P, P], BF16, name="hidden_t")
             nc.tensor.transpose(bias_cols_ps[:], bias_rows[:], ident[:])
@@ -191,7 +161,10 @@ def tile_syntacticgcn_kernel(
                 nc.tensor.transpose(
                     bias_ps[:, c * P : (c + 1) * P], bias_cols[:, c : c + 1].to_broadcast([P, P]), ident[:]
                 )
-            nc.vector.tensor_copy(out=bias_all[:], in_=bias_ps[:])
+            bspread_ps[0] = bias_ps
+
+        def copy_bias():
+            nc.vector.tensor_copy(out=bias_all[:], in_=bspread_ps[0][:])
 
         for item in LOADS.split():
             if item == "small":
@@ -208,6 +181,7 @@ def tile_syntacticgcn_kernel(
 
         partial_of = {}
         masked_of = {}
+        cnt_of = {}
         alo_of = {}
         or_of = {}
         row_abs_of = {}
@@ -229,7 +203,7 @@ def tile_syntacticgcn_kernel(
             return nc.gpsimd if (i, which) in GPSIMD_TREES else nc.vector
 
         def chunk_of(i, which):
-            return CHUNK if (i, which) in GPSIMD_TREES else SLOTS // 4
+            return CHUNK if (i, which) in GPSIMD_TREES or (i, which) in HALF_TREES else SLOTS // 4
 
         def add_quarter(i, which, q):
             tile = (src_tiles if which == 0 else neigh_tiles)[i]
@@ -287,10 +261,16 @@ def tile_syntacticgcn_kernel(
             valid = work.tile([P, SLOTS], F32)
             count = work.tile([P, 1], F32)
             nc.scalar.activation(out=valid[:], in_=row_abs_of[i][:], func=ACT.Sign, accum_out=count[:])
+            cnt_of[i] = count
+
+        def imax(i):
             at_least_one = work.tile([P, 1], F32)
-            nc.vector.tensor_scalar_max(out=at_least_one[:], in0=count[:], scalar1=1.0)
+            nc.vector.tensor_scalar_max(out=at_least_one[:], in0=cnt_of[i][:], scalar1=1.0)
+            alo_of[i] = at_least_one
+
+        def irec(i):
             inv_count = const.tile([P, 1], F32, name="inv_count_kept%d" % i)
-            nc.vector.reciprocal(out=inv_count[:], in_=at_least_one[:])
+            nc.vector.reciprocal(out=inv_count[:], in_=alo_of[i][:])
             inv_count_of[i] = inv_count
 
         def count_on_tensor(i):
@@ -337,7 +317,7 @@ def tile_syntacticgcn_kernel(
             nc.tensor.transpose(small_ps_of[i][:, 0:P], factor_rows[i % 2][:], ident_f32[:])
 
         def copy_factor(i):
-            factor = work.tile([P, P], F32)
+            factor = work.tile([P, P], F32, bufs=3)
             nc.vector.tensor_copy(out=factor[:], in_=small_ps_of[i][:, 0:P])
             factor_of[i] = factor
 
@@ -357,7 +337,7 @@ def tile_syntacticgcn_kernel(
                     )
 
         def scale_and_group(i):
-            grouped = work.tile([P, P, PACK], BF16, align_bytes=64)
+            grouped = work.tile([P, P, PACK], BF16, bufs=4, align_bytes=64)
             nc.vector.tensor_tensor(
                 out=grouped[:],
                 in0=hidden_ps_of[i][:].rearrange("p t n -> p n t"),
@@ -390,13 +370,13 @@ def tile_syntacticgcn_kernel(
             hidden_ps_of[i] = hidden_t
 
         def group_only(i):
-            grouped = work.tile([P, P, PACK], BF16, align_bytes=64)
+            grouped = work.tile([P, P, PACK], BF16, bufs=4, align_bytes=64)
             nc.scalar.copy(out=grouped[:], in_=hidden_ps_of[i][:].rearrange("p t n -> p n t"))
             grouped_of[i] = grouped
 
         def quantise(i):
-            codes = work.tile([P, P], U32, align_bytes=64)
-            scales = work.tile([P, P], U8, align_bytes=64)
+            codes = work.tile([P, P], U32, bufs=4, align_bytes=64)
+            scales = work.tile([P, P], U8, bufs=4, align_bytes=64)
             nc.vector.quantize_mx(
                 out=codes[:].bitcast(FP8X4),
                 scales=scales[:],
@@ -444,6 +424,16 @@ def tile_syntacticgcn_kernel(
             )
             nc.sync.dma_start(out=out[i * P : (i + 1) * P, cols], in_=result[:, cols])
 
+        def gleaky(i, h):
+            cols = slice(h * N_TILE, (h + 1) * N_TILE)
+            result = result_of[i]
+            below = work.tile([P, N_TILE], F32)
+            nc.gpsimd.tensor_scalar(
+                out=below[:], in0=result[:, cols], scalar1=0.0, scalar2=NEG_SLOPE - 1.0, op0=ALU.min, op1=ALU.mult
+            )
+            nc.gpsimd.tensor_tensor(out=result[:, cols], in0=result[:, cols], in1=below[:], op=ALU.add)
+            nc.sync.dma_start(out=out[i * P : (i + 1) * P, cols], in_=result[:, cols])
+
         def finish(i):
             add_bias(i, 0)
             add_bias(i, 1)
@@ -458,7 +448,9 @@ def tile_syntacticgcn_kernel(
             "quarter": add_quarter,
             "fold": fold,
             "tree": tree,
-            "inv": invert_count_of_rows,
+            "sgn": invert_count_of_rows,
+            "imax": imax,
+            "irec": irec,
             "rows": rows_to_hidden_ps,
             "group": group_only,
             "quant": quantise,
@@ -474,8 +466,10 @@ def tile_syntacticgcn_kernel(
             "scale": scale_and_group,
             "add": add_bias,
             "leaky": leaky_and_store,
+            "gleaky": gleaky,
             "bcols": bias_to_columns,
             "bspread": spread_bias,
+            "bcopy": copy_bias,
         }
         with tc.manual_schedule():
             for word in ORDER.split():

@@ -35,29 +35,26 @@ ROW_TILES = (0, 1, 2,)
 GPSIMD_TREES = ()
 HALF_TREES = ((0, 1),)
 CHUNK = 2
-LOADS = "n0x4 s0 small n1 s1 n2 s2 n3 s3 w n4 s4x2 n5 n6 s5x4 n7x2 s6x4 s7x4"
+LOADS = "n0x4 s0 small n1 s1 n2 s2 n3 s3 w n4 s4x2 n5 s5x4:01 n6 s5x4:23 s6x4:01 n7x2 s6x4:23 s7x4"
 ORDER = """
 
 tests:0,0,16 sgn:0
-quarter:0,1,1 quarter:0,1,2 quarter:0,1,3 quarter:0,0,1 fold:0,1,2 quarter:0,0,2 fold:0,1,1 quarter:0,0,3 bcols bspread fold:0,0,2
-tests:1,0,16 sgn:1
-quarter:1,1,1 fold:0,0,1 quarter:1,0,1 imax:0 quarter:1,1,2 irec:0 rows:0 quarter:1,0,2 quarter:1,1,3 quarter:1,0,3 fold:1,1,2 fold:1,0,2 bcopy fold:1,1,1 fold:1,0,1
+quarter:0,1,1 quarter:0,1,2 quarter:0,1,3 quarter:0,0,1 bcols bspread bcopy tests:1,0,16 sgn:1 fold:0,1,2 quarter:0,0,2 fold:0,1,1 imax:0 quarter:0,0,3 irec:0 quarter:1,1,1 fold:0,0,2 nrow:0
+quarter:1,0,1 srow:0 rows:0 quarter:1,1,2 quarter:1,0,2 quarter:1,1,3 quarter:1,0,3 fold:1,1,2 fold:1,0,2 fold:1,1,1
 tests:2,0,16 sgn:2
-tests:3,0,5 group:0 tests:3,5,16
-quarter:2,1,1 imax:1 quarter:2,0,1 irec:1 sum:3,0,16 quarter:2,1,2 quarter:2,0,2 quant:0 mul:0 rows:1 quarter:2,1,3 mask:3 cnt:3 quarter:2,0,3 fmax:3 fold:2,1,2 frecip:3 imax:2 fold:2,0,2 irec:2 fspread:3 ft:3 fold:2,1,1 fold:2,0,1 fcopy:3
+tests:3,0,2 group:0 tests:3,2,16
+imax:1 srow:1 irec:1 quarter:2,1,1 nrow:1 rows:1 quarter:2,0,1 sum:3,0,16 quarter:2,1,2 quarter:2,0,2 quant:0 mul:0 quarter:2,1,3 quarter:2,0,3 mask:3 cnt:3 fold:2,1,2 imax:2 fold:2,0,2 fmax:3 irec:2 frecip:3 fold:2,1,1 fspread:3 ft:3 srow:2 add:0,0 fcopy:3 nrow:2
 sum:4,0,8
-tests:4,0,9 group:1 tests:4,9,16
-tests:5,0,4
-scale:3 add:0,0 quant:3 rows:2 mul:3 group:2 tests:5,4,16
-add:0,1 quant:1 leaky:0,0 mask:4 cnt:4 mul:1 sum:4,8,16 leaky:0,1 
+tests:4,0,2 group:1 tests:4,2,16
+tests:5,0,2
+rows:2 group:2 tests:5,2,16
 tests:6,0,16
-add:3,0 fmax:4 add:3,1 frecip:4 leaky:3,0 fspread:4 ft:4 quant:2 mul:2 leaky:3,1 fcopy:4 add:1,0 scale:4 add:1,1 quant:4 sum:5,0,4 sum:5,4,8  mul:4 leaky:1,0 leaky:1,1
-mask:5 cnt:5 sum:5,8,12 sum:5,12,16 
+scale:3 add:0,1 quant:3 mul:3 leaky:0 quant:1 mask:4 sum:4,8,12 cnt:4 sum:4,12,16 mul:1
+
+add:3,0 add:3,1 fmax:4 leaky:3,0 frecip:4 leaky:3,1 fspread:4 ft:4 add:1,0 add:1,1 fcopy:4 quant:2 sum:5,0,4 sum:5,4,8  mul:2 scale:4 leaky:1,0 quant:4 mul:4 leaky:1,1 mask:5 cnt:5 sum:5,8,12 sum:5,12,16  
 tests:7,0,16
-
-add:4,0 fmax:5 add:4,1 frecip:5 leaky:4,0 fspread:5 ft:5 leaky:4,1 fcopy:5 sum:6,0,4  add:2,0 scale:5 mask:6 cnt:6 quant:5 add:2,1 fmax:6 sum:6,4,8 sum:6,8,12  leaky:2,0 frecip:6 mul:5 leaky:2,1 fspread:6 ft:6 sum:6,12,16  add:5,0 fcopy:6 add:5,1 sum:7,0,4 sum:7,4,8  leaky:5,0 scale:6
-mask:7 cnt:7 quant:6 mul:6,0,1 leaky:5,1 fmax:7 frecip:7 sum:7,8,12  fspread:7 ft:7 sum:7,12,16  mul:6,1,2 add:6,0 fcopy:7 leaky:6,0 scale:7 add:6,1 quant:7 mul:7 leaky:6,1 add:7,0 add:7,1 leaky:7,0 leaky:7,1
-
+add:2,0 add:4,0 fmax:5 add:4,1 frecip:5 leaky:4,0 fspread:5 sum:6,0,4  ft:5 leaky:4,1 fcopy:5 add:2,1 scale:5 sum:6,4,8  mask:6 cnt:6 quant:5 mul:5 leaky:2,0 fmax:6 leaky:2,1 frecip:6 sum:6,8,12  fspread:6 ft:6 sum:6,12,16  add:5,0 fcopy:6 add:5,1 sum:7,0,4 sum:7,4,8  leaky:5,0 scale:6
+mask:7 cnt:7 quant:6 mul:6,0,1 leaky:5,1 fmax:7 frecip:7 fspread:7 sum:7,8,12  ft:7 sum:7,12,16  mul:6,1,2 add:6,0 fcopy:7 leaky:6,0 scale:7 add:6,1 quant:7 mul:7 leaky:6,1 add:7,0 add:7,1 leaky:7,0 leaky:7,1
 """
 
 FLOPS = 2 * NODE_TILES * P * K * H
@@ -109,7 +106,7 @@ def tile_syntacticgcn_kernel(
         def by_slot(features):
             return features.rearrange("s m d -> (s m) d").rearrange("(g p) d -> p g d", p=P)
 
-        def load(kind, i, pieces=1, queue=nc.sync):
+        def load(kind, i, pieces=1, queue=nc.sync, part=None):
             features = (src_node_features if kind == "s" else neigh_node_features)[i]
             if on_rows(i):
                 tiles = src_tiles if kind == "s" else neigh_tiles
@@ -125,6 +122,8 @@ def tile_syntacticgcn_kernel(
                 cols = slice(0, FEAT) if kind == "s" else slice(FEAT, K)
                 step = GROUPS // pieces
                 for g in range(0, GROUPS, step):
+                    if part is not None and g // step not in part:
+                        continue
                     queue.dma_start(
                         out=both_tiles[i][:, g : g + step, cols], in_=by_slot(features)[:, g : g + step, :]
                     )
@@ -151,8 +150,8 @@ def tile_syntacticgcn_kernel(
         bspread_ps = {}
 
         def bias_to_columns():
-            bias_cols_ps = psum.tile([P, P], BF16, name="hidden_t")
-            nc.tensor.transpose(bias_cols_ps[:], bias_rows[:], ident[:])
+            bias_cols_ps = psum.tile([P, H], BF16, name="small", bufs=2)
+            nc.tensor.transpose(bias_cols_ps[:, 0:P], bias_rows[:], ident[:])
             nc.vector.tensor_copy(out=bias_cols[:], in_=bias_cols_ps[:, 0:H_BLOCKS])
 
         def spread_bias():
@@ -164,7 +163,7 @@ def tile_syntacticgcn_kernel(
             bspread_ps[0] = bias_ps
 
         def copy_bias():
-            nc.vector.tensor_copy(out=bias_all[:], in_=bspread_ps[0][:])
+            nc.scalar.copy(out=bias_all[:], in_=bspread_ps[0][:])
 
         for item in LOADS.split():
             if item == "small":
@@ -176,12 +175,13 @@ def tile_syntacticgcn_kernel(
                     item[0],
                     int(item[1]),
                     int(item[3]) if len(item) > 2 else 1,
-                    nc.scalar if item[len(item) - 1] == "A" else nc.sync,
+                    part=[int(x) for x in item.split(":")[1]] if ":" in item else None,
                 )
 
         partial_of = {}
         masked_of = {}
         cnt_of = {}
+        hidden_of = {}
         alo_of = {}
         or_of = {}
         row_abs_of = {}
@@ -210,7 +210,7 @@ def tile_syntacticgcn_kernel(
             quarter = SLOTS // 4
             if q == 1:
                 tag = "partial%d%s" % (which, "g" if (i, which) in GPSIMD_TREES else "v")
-                partial = work.tile([P, quarter, FEAT], F32, name=tag)
+                partial = work.tile([P, quarter, FEAT], F32, name=tag, bufs=3)
                 partial_of[(i, which)] = partial
             partial = partial_of[(i, which)]
             for m in range(0, quarter, chunk_of(i, which)):
@@ -263,6 +263,16 @@ def tile_syntacticgcn_kernel(
             nc.scalar.activation(out=valid[:], in_=row_abs_of[i][:], func=ACT.Sign, accum_out=count[:])
             cnt_of[i] = count
 
+        def test_rows_vector(i, first, last):
+            for r in range(first, last):
+                nc.vector.tensor_reduce(
+                    out=row_abs_of[i][:, r : r + 1],
+                    in_=neigh_row(i, r),
+                    axis=AX.X,
+                    op=ALU.max,
+                    apply_absolute_value=True,
+                )
+
         def imax(i):
             at_least_one = work.tile([P, 1], F32)
             nc.vector.tensor_scalar_max(out=at_least_one[:], in0=cnt_of[i][:], scalar1=1.0)
@@ -287,7 +297,7 @@ def tile_syntacticgcn_kernel(
 
         def count_matmul(i):
             masked = masked_of[i]
-            small_ps = psum.tile([P, P + 1], F32)
+            small_ps = psum.tile([P, N_TILE], F32, name="small", bufs=2)
             nc.tensor.matmul(
                 out=small_ps[:, P : P + 1],
                 lhsT=masked[:].rearrange("q g n -> q (g n)"),
@@ -346,32 +356,42 @@ def tile_syntacticgcn_kernel(
             )
             grouped_of[i] = grouped
 
-        def rows_to_hidden_ps(i):
-            hidden = work.tile([P, PACK, P], BF16)
-            nc.gpsimd.tensor_scalar(
+        def new_hidden(i):
+            if i not in hidden_of:
+                hidden = work.tile([P, PACK, P], BF16)
+                hidden_of[i] = hidden
+
+        def source_row(i):
+            new_hidden(i)
+            hidden = hidden_of[i]
+            partial = partial_of[(i, 0)]
+            nc.vector.tensor_tensor(
                 out=hidden[:, :, 0:SRC_P],
-                in0=partial_of[(i, 0)][:, 0, :].rearrange("n (p t) -> n t p", t=PACK),
-                scalar1=1.0,
-                scalar2=0.0,
-                op0=ALU.mult,
-                op1=ALU.add,
+                in0=partial[:, 0, :].rearrange("n (p t) -> n t p", t=PACK),
+                in1=partial[:, 1, :].rearrange("n (p t) -> n t p", t=PACK),
+                op=ALU.add,
             )
-            nc.gpsimd.tensor_scalar(
-                out=hidden[:, :, SRC_P:P],
+
+        def neigh_row_mean(i):
+            new_hidden(i)
+            nc.vector.tensor_scalar(
+                out=hidden_of[i][:, :, SRC_P:P],
                 in0=partial_of[(i, 1)][:, 0, :].rearrange("n (p t) -> n t p", t=PACK),
                 scalar1=inv_count_of[i][:, 0:1],
-                scalar2=0.0,
+                scalar2=None,
                 op0=ALU.mult,
-                op1=ALU.add,
             )
-            hidden_t = psum.tile([P, PACK, P], BF16)
+
+        def rows_to_hidden_ps(i):
+            hidden = hidden_of[i]
+            hidden_t = psum.tile([P, 2 * PACK, P], BF16, name="small", bufs=2)
             for t in range(PACK):
                 nc.tensor.transpose(hidden_t[:, t, :], hidden[:, t, :], ident[:])
             hidden_ps_of[i] = hidden_t
 
         def group_only(i):
             grouped = work.tile([P, P, PACK], BF16, bufs=4, align_bytes=64)
-            nc.scalar.copy(out=grouped[:], in_=hidden_ps_of[i][:].rearrange("p t n -> p n t"))
+            nc.scalar.copy(out=grouped[:], in_=hidden_ps_of[i][:, 0:PACK, :].rearrange("p t n -> p n t"))
             grouped_of[i] = grouped
 
         def quantise(i):
@@ -411,8 +431,8 @@ def tile_syntacticgcn_kernel(
                 out=result_of[i][:, cols], in0=acc_of[i][h][:], in1=bias_all[:, cols], op=ALU.add
             )
 
-        def leaky_and_store(i, h):
-            cols = slice(h * N_TILE, (h + 1) * N_TILE)
+        def leaky_and_store(i, h=None):
+            cols = slice(0, H) if h is None else slice(h * N_TILE, (h + 1) * N_TILE)
             result = result_of[i]
             nc.vector.scalar_tensor_tensor(
                 out=result[:, cols],
@@ -424,14 +444,14 @@ def tile_syntacticgcn_kernel(
             )
             nc.sync.dma_start(out=out[i * P : (i + 1) * P, cols], in_=result[:, cols])
 
-        def gleaky(i, h):
-            cols = slice(h * N_TILE, (h + 1) * N_TILE)
+        def gleaky(i, h=None):
+            cols = slice(0, H) if h is None else slice(h * N_TILE, (h + 1) * N_TILE)
             result = result_of[i]
-            below = work.tile([P, N_TILE], F32)
+            below = work.tile([P, H], F32, bufs=1)
             nc.gpsimd.tensor_scalar(
-                out=below[:], in0=result[:, cols], scalar1=0.0, scalar2=NEG_SLOPE - 1.0, op0=ALU.min, op1=ALU.mult
+                out=below[:, cols], in0=result[:, cols], scalar1=0.0, scalar2=NEG_SLOPE - 1.0, op0=ALU.min, op1=ALU.mult
             )
-            nc.gpsimd.tensor_tensor(out=result[:, cols], in0=result[:, cols], in1=below[:], op=ALU.add)
+            nc.gpsimd.tensor_tensor(out=result[:, cols], in0=result[:, cols], in1=below[:, cols], op=ALU.add)
             nc.sync.dma_start(out=out[i * P : (i + 1) * P, cols], in_=result[:, cols])
 
         def finish(i):
@@ -442,6 +462,7 @@ def tile_syntacticgcn_kernel(
 
         verbs = {
             "tests": test_rows_scalar,
+            "vtests": test_rows_vector,
             "ssrc": lambda i, pieces: load("s", i, pieces, nc.scalar),
             "gsrc": lambda i, pieces: load("s", i, pieces, nc.gpsimd),
             "trees": two_trees,
@@ -451,6 +472,8 @@ def tile_syntacticgcn_kernel(
             "sgn": invert_count_of_rows,
             "imax": imax,
             "irec": irec,
+            "srow": source_row,
+            "nrow": neigh_row_mean,
             "rows": rows_to_hidden_ps,
             "group": group_only,
             "quant": quantise,

@@ -34,27 +34,30 @@ OR_STOP = 8
 ROW_TILES = (0, 1, 2,)
 GPSIMD_TREES = ()
 HALF_TREES = ((0, 1),)
+SCALAR_FACTOR = (7,)
+FULL_STORE = (0, 1, 2, 3, 4, 5,)
 CHUNK = 2
-LOADS = "n0x4 s0 small n1 s1 n2 s2 n3 s3 w n4 s4x2 n5 s5x4:01 n6 s5x4:23 s6x4:01 n7x2 s6x4:23 s7x4"
+TINY = 2.0 ** -107
+LOADS = "n0x4 s0x2:0 n1x2:0 s0x2:1 n1x2:1 small s1 n2 s2 n3 s3 w n4 s4x2:0 n5 s4x2:1 s5x4:01 n6x2 s5x4:23 s6x4:01 n7x2 s6x4:23 s7x4"
 ORDER = """
 
 tests:0,0,16 sgn:0
-quarter:0,1,1 quarter:0,1,2 quarter:0,1,3 quarter:0,0,1 bcols bspread bcopy tests:1,0,16 sgn:1 fold:0,1,2 quarter:0,0,2 fold:0,1,1 imax:0 quarter:0,0,3 irec:0 quarter:1,1,1 fold:0,0,2 nrow:0
+quarter:0,1,1 quarter:0,1,2 quarter:0,1,3 quarter:0,0,1 fold:0,1,2 quarter:0,0,2 fold:0,1,1 imax:0 quarter:0,0,3 bcols bspread tests:1,0,16 sgn:1 bcopy irec:0 quarter:1,1,1 fold:0,0,2 nrow:0
 quarter:1,0,1 srow:0 rows:0 quarter:1,1,2 quarter:1,0,2 quarter:1,1,3 quarter:1,0,3 fold:1,1,2 fold:1,0,2 fold:1,1,1
 tests:2,0,16 sgn:2
 tests:3,0,2 group:0 tests:3,2,16
-imax:1 srow:1 irec:1 quarter:2,1,1 nrow:1 rows:1 quarter:2,0,1 sum:3,0,16 quarter:2,1,2 quarter:2,0,2 quant:0 mul:0 quarter:2,1,3 quarter:2,0,3 mask:3 cnt:3 fold:2,1,2 imax:2 fold:2,0,2 fmax:3 irec:2 frecip:3 fold:2,1,1 fspread:3 ft:3 srow:2 add:0,0 fcopy:3 nrow:2
+imax:1 srow:1 irec:1 quarter:2,1,1 nrow:1 rows:1 quarter:2,0,1 sum:3,0,16 quarter:2,1,2 quarter:2,0,2 quant:0 quarter:2,1,3 quarter:2,0,3 mask:3 cnt:3 mul:0 fold:2,1,2 imax:2 fold:2,0,2 irec:2 frecip:3 fold:2,1,1 fspread:3 ft:3 srow:2 add:0,0 fcopy:3 nrow:2
 sum:4,0,8
 tests:4,0,2 group:1 tests:4,2,16
 tests:5,0,2
 rows:2 group:2 tests:5,2,16
 tests:6,0,16
-scale:3 add:0,1 quant:3 mul:3 leaky:0 quant:1 mask:4 sum:4,8,12 cnt:4 sum:4,12,16 mul:1
+scale:3 add:0,1 quant:3 mul:3 leaky:0 quant:1 mul:1 mask:4 cnt:4 sum:4,8,16
 
-add:3,0 add:3,1 fmax:4 leaky:3,0 frecip:4 leaky:3,1 fspread:4 ft:4 add:1,0 add:1,1 fcopy:4 quant:2 sum:5,0,4 sum:5,4,8  mul:2 scale:4 leaky:1,0 quant:4 mul:4 leaky:1,1 mask:5 cnt:5 sum:5,8,12 sum:5,12,16  
+add:3,0 add:3,1 frecip:4 leaky:3,0 fspread:4 ft:4 leaky:3,1 add:1,0 fcopy:4 quant:2 sum:5,0,4 sum:5,4,8  add:1,1 scale:4 mul:2 leaky:1,0 quant:4 mul:4 leaky:1,1 mask:5 cnt:5 sum:5,8,12  
 tests:7,0,16
-add:2,0 add:4,0 fmax:5 add:4,1 frecip:5 leaky:4,0 fspread:5 sum:6,0,4  ft:5 leaky:4,1 fcopy:5 add:2,1 scale:5 sum:6,4,8  mask:6 cnt:6 quant:5 mul:5 leaky:2,0 fmax:6 leaky:2,1 frecip:6 sum:6,8,12  fspread:6 ft:6 sum:6,12,16  add:5,0 fcopy:6 add:5,1 sum:7,0,4 sum:7,4,8  leaky:5,0 scale:6
-mask:7 cnt:7 quant:6 mul:6,0,1 leaky:5,1 fmax:7 frecip:7 fspread:7 sum:7,8,12  ft:7 sum:7,12,16  mul:6,1,2 add:6,0 fcopy:7 leaky:6,0 scale:7 add:6,1 quant:7 mul:7 leaky:6,1 add:7,0 add:7,1 leaky:7,0 leaky:7,1
+add:2,0 add:4,0 frecip:5 add:4,1 fspread:5 ft:5 sum:5,12,16  sum:6,0,4 sum:6,4,8  leaky:4,0 fcopy:5 add:2,1 scale:5 leaky:4,1 mask:6 cnt:6 quant:5 mul:5 leaky:2,0 frecip:6 leaky:2,1 fspread:6 ft:6 sum:6,8,12 sum:6,12,16  add:5,0 fcopy:6 add:5,1 sum:7,0,4 sum:7,4,8  leaky:5,0 scale:6
+mask:7 cnt:7 quant:6 mul:6,0,1 leaky:5,1 frecip:7 fspread:7 sum:7,8,12  ft:7 fcopy:7 sum:7,12,16  mul:6,1,2 add:6,0 leaky:6,0 scale:7 add:6,1 quant:7 mul:7 leaky:6,1 add:7,0 add:7,1 leaky:7,0 leaky:7,1
 """
 
 FLOPS = 2 * NODE_TILES * P * K * H
@@ -93,6 +96,8 @@ def tile_syntacticgcn_kernel(
         nc.vector.tensor_copy(out=slot_sum[:], in_=slot_sum_f32[:])
         ones_col = const.tile([P, 1], BF16)
         nc.vector.memset(ones_col[:], 1.0)
+        tiny = const.tile([P, P], BF16)
+        nc.vector.memset(tiny[:], TINY)
         factor_rows = []
         for j in range(2):
             factor_row = const.tile([P, P], F32, name="factor_rows%d" % j)
@@ -110,11 +115,15 @@ def tile_syntacticgcn_kernel(
             features = (src_node_features if kind == "s" else neigh_node_features)[i]
             if on_rows(i):
                 tiles = src_tiles if kind == "s" else neigh_tiles
-                tile = inputs.tile([P, SLOTS, FEAT], BF16, name="%s%d" % (kind, i))
+                if i not in tiles:
+                    tile = inputs.tile([P, SLOTS, FEAT], BF16, name="%s%d" % (kind, i))
+                    tiles[i] = tile
+                tile = tiles[i]
                 step = SLOTS // pieces
                 for m in range(0, SLOTS, step):
+                    if part is not None and m // step not in part:
+                        continue
                     nc.sync.dma_start(out=tile[:, m : m + step, :], in_=features[:, m : m + step, :])
-                tiles[i] = tile
             else:
                 if i not in both_tiles:
                     both = inputs.tile([P, GROUPS, K], BF16, name="both%d" % i)
@@ -303,7 +312,10 @@ def tile_syntacticgcn_kernel(
                 lhsT=masked[:].rearrange("q g n -> q (g n)"),
                 rhs=ones_col[:],
                 start=True,
-                stop=True,
+                stop=False,
+            )
+            nc.tensor.matmul(
+                out=small_ps[:, P : P + 1], lhsT=tiny[:], rhs=ones_col[:], start=False, stop=True
             )
             small_ps_of[i] = small_ps
 
@@ -314,7 +326,7 @@ def tile_syntacticgcn_kernel(
 
         def frecip(i):
             inv_count = work.tile([P, 1], F32)
-            nc.vector.reciprocal(out=inv_count[:], in_=alo_of[i][:])
+            nc.vector.reciprocal(out=inv_count[:], in_=small_ps_of[i][:, P : P + 1])
             inv_count_of[i] = inv_count
 
         def fspread(i):
@@ -328,7 +340,7 @@ def tile_syntacticgcn_kernel(
 
         def copy_factor(i):
             factor = work.tile([P, P], F32, bufs=3)
-            nc.vector.tensor_copy(out=factor[:], in_=small_ps_of[i][:, 0:P])
+            (nc.scalar.copy if i in SCALAR_FACTOR else nc.vector.tensor_copy)(out=factor[:], in_=small_ps_of[i][:, 0:P])
             factor_of[i] = factor
 
         def sum_on_tensor(i, first, last):
@@ -442,7 +454,11 @@ def tile_syntacticgcn_kernel(
                 op0=ALU.mult,
                 op1=ALU.max,
             )
-            nc.sync.dma_start(out=out[i * P : (i + 1) * P, cols], in_=result[:, cols])
+            if i in FULL_STORE:
+                if h != 0:
+                    nc.sync.dma_start(out=out[i * P : (i + 1) * P, :], in_=result[:])
+            else:
+                nc.sync.dma_start(out=out[i * P : (i + 1) * P, cols], in_=result[:, cols])
 
         def gleaky(i, h=None):
             cols = slice(0, H) if h is None else slice(h * N_TILE, (h + 1) * N_TILE)

@@ -33,12 +33,12 @@ OR_STOP = 8
 
 ROW_TILES = (0, 1, 2,)
 GPSIMD_TREES = ()
-HALF_TREES = ((0, 1),)
+HALF_TREES = ()
 SCALAR_FACTOR = (7,)
 FULL_STORE = (0, 1, 2, 3, 4, 5,)
 CHUNK = 2
 TINY = 2.0 ** -107
-LOADS = "n0x4 s0x2:0 n1x2:0 s0x2:1 n1x2:1 small s1 n2 s2 n3 s3 w n4 s4x2:0 n5 s4x2:1 s5x4:01 n6x2 s5x4:23 s6x4:01 n7x2 s6x4:23 s7x4"
+LOADS = "n0x2 s0 n1 small s1 n2 s2 n3 s3 w n4 s4x2:0 n5 s4x2:1 s5x2:0 n6 s5x2:1 s6x2:0 n7x2 s6x2:1 s7x2"
 ORDER = """
 
 tests:0,0,16 sgn:0
@@ -384,6 +384,15 @@ def tile_syntacticgcn_kernel(
                 op=ALU.add,
             )
 
+        def neigh_row_scalar(i):
+            new_hidden(i)
+            nc.scalar.activation(
+                out=hidden_of[i][:, :, SRC_P:P],
+                in_=partial_of[(i, 1)][:, 0, :].rearrange("n (p t) -> n t p", t=PACK),
+                func=ACT.Copy,
+                scale=inv_count_of[i][:, 0:1],
+            )
+
         def neigh_row_mean(i):
             new_hidden(i)
             nc.vector.tensor_scalar(
@@ -460,6 +469,14 @@ def tile_syntacticgcn_kernel(
             else:
                 nc.sync.dma_start(out=out[i * P : (i + 1) * P, cols], in_=result[:, cols])
 
+        def leaky_piece(i, q):
+            cols = slice(q * FEAT, (q + 1) * FEAT)
+            result = result_of[i]
+            nc.vector.scalar_tensor_tensor(
+                out=result[:, cols], in0=result[:, cols], scalar=NEG_SLOPE, in1=result[:, cols], op0=ALU.mult, op1=ALU.max
+            )
+            nc.sync.dma_start(out=out[i * P : (i + 1) * P, cols], in_=result[:, cols])
+
         def gleaky(i, h=None):
             cols = slice(0, H) if h is None else slice(h * N_TILE, (h + 1) * N_TILE)
             result = result_of[i]
@@ -490,6 +507,8 @@ def tile_syntacticgcn_kernel(
             "irec": irec,
             "srow": source_row,
             "nrow": neigh_row_mean,
+            "nrowA": neigh_row_scalar,
+            "leaky2": leaky_piece,
             "rows": rows_to_hidden_ps,
             "group": group_only,
             "quant": quantise,

from contextlib import ExitStack

import concourse.mybir as mybir
from concourse.masks import make_identity

F32 = mybir.dt.float32
BF16 = mybir.dt.bfloat16
I32 = mybir.dt.int32
U32 = mybir.dt.uint32
U8 = mybir.dt.uint8
FP8X4 = mybir.dt.float8_e4m3fn_x4
ALU = mybir.AluOpType
ACT = mybir.ActivationFunctionType
AX = mybir.AxisListType

P = 128
PACK = 4
NODE_TILES = 8
SLOTS = 16
FEAT = 256
K = 2 * FEAT
H = 1024
N_TILE = 512
H_BLOCKS = H // P
GROUP = P // SLOTS
GROUPS = P // GROUP
SRC_P = FEAT // PACK
NEG_SLOPE = 0.01
FIRST_LOAD_PIECES = 4
WORDS = FEAT // 2
MAGNITUDE_BITS = 0x7FFF7FFF
OR_STOP = 8

ROW_TILES = (0, 1, 2,)
GPSIMD_TREES = ()
HALF_TREES = ()
SCALAR_FACTOR = (7,)
FULL_STORE = (0, 1, 2, 3, 4, 5,)
CHUNK = 2
TINY = 2.0 ** -107
LOADS = "n0x2 s0 n1 small s1 n2 s2 n3 s3 w n4 s4x2:0 n5 s4x2:1 s5x2:0 n6 s5x2:1 s6x2:0 n7x2 s6x2:1 s7x2"
ORDER = """

tests:0,0,16 sgn:0
quarter:0,1,1 quarter:0,1,2 quarter:0,1,3 quarter:0,0,1 fold:0,1,2 quarter:0,0,2 fold:0,1,1 imax:0 quarter:0,0,3 bcols bspread tests:1,0,16 sgn:1 bcopy irec:0 quarter:1,1,1 fold:0,0,2 nrow:0
quarter:1,0,1 srow:0 rows:0 quarter:1,1,2 quarter:1,0,2 quarter:1,1,3 quarter:1,0,3 fold:1,1,2 fold:1,0,2 fold:1,1,1
tests:2,0,16 sgn:2
tests:3,0,2 group:0 tests:3,2,16
imax:1 srow:1 irec:1 quarter:2,1,1 nrow:1 rows:1 quarter:2,0,1 sum:3,0,16 quarter:2,1,2 quarter:2,0,2 quant:0 quarter:2,1,3 quarter:2,0,3 mask:3 cnt:3 mul:0 fold:2,1,2 imax:2 fold:2,0,2 irec:2 frecip:3 fold:2,1,1 fspread:3 ft:3 srow:2 add:0,0 fcopy:3 nrow:2
sum:4,0,8
tests:4,0,2 group:1 tests:4,2,16
tests:5,0,2
rows:2 group:2 tests:5,2,16
tests:6,0,16
scale:3 add:0,1 quant:3 mul:3 leaky:0 quant:1 mul:1 mask:4 cnt:4 sum:4,8,16

add:3,0 add:3,1 frecip:4 leaky:3,0 fspread:4 ft:4 leaky:3,1 add:1,0 fcopy:4 quant:2 sum:5,0,4 sum:5,4,8  add:1,1 scale:4 mul:2 leaky:1,0 quant:4 mul:4 leaky:1,1 mask:5 cnt:5 sum:5,8,12  
tests:7,0,16
add:2,0 add:4,0 frecip:5 add:4,1 fspread:5 ft:5 sum:5,12,16  sum:6,0,4 sum:6,4,8  leaky:4,0 fcopy:5 add:2,1 scale:5 leaky:4,1 mask:6 cnt:6 quant:5 mul:5 leaky:2,0 frecip:6 leaky:2,1 fspread:6 ft:6 sum:6,8,12 sum:6,12,16  add:5,0 fcopy:6 add:5,1 sum:7,0,4 sum:7,4,8  leaky:5,0 scale:6
mask:7 cnt:7 quant:6 mul:6,0,1 leaky:5,1 frecip:7 fspread:7 sum:7,8,12  ft:7 fcopy:7 sum:7,12,16  mul:6,1,2 add:6,0 leaky:6,0 scale:7 add:6,1 quant:7 mul:7 leaky:6,1 add:7,0 add:7,1 leaky:7,0 leaky:7,1
"""

FLOPS = 2 * NODE_TILES * P * K * H


def tile_syntacticgcn_kernel(
    tc, src_node_features, neigh_node_features, W_map_words, W_map_scales, b_map, out
):
    nc = tc.nc
    with ExitStack() as ctx:
        const = ctx.enter_context(tc.tile_pool(name="const", bufs=1))
        inputs = ctx.enter_context(tc.tile_pool(name="inputs", bufs=1))
        work = ctx.enter_context(tc.tile_pool(name="work", bufs=2))
        results = ctx.enter_context(tc.tile_pool(name="results", bufs=NODE_TILES))
        psum = ctx.enter_context(tc.psum_pool(name="psum", bufs=1))

        def on_rows(i):
            return i in ROW_TILES

        w_scales = const.tile([P, H], U8, align_bytes=64)
        nc.vector.memset(w_scales[:].bitcast(I32), 0)
        bias_rows = const.tile([P, P], BF16)
        nc.gpsimd.memset(bias_rows[:], 0.0)
        ident = const.tile([P, P], BF16)
        make_identity(nc, ident[:])
        ident_f32 = const.tile([P, P], F32)
        make_identity(nc, ident_f32[:])
        slot_sum_f32 = const.tile([P, GROUP], F32)
        nc.vector.tensor_reduce(
            out=slot_sum_f32[:],
            in_=ident[:].rearrange("p (n m) -> p n m", m=SLOTS),
            axis=AX.X,
            op=ALU.add,
        )
        slot_sum = const.tile([P, GROUP], BF16)
        nc.vector.tensor_copy(out=slot_sum[:], in_=slot_sum_f32[:])
        ones_col = const.tile([P, 1], BF16)
        nc.vector.memset(ones_col[:], 1.0)
        tiny = const.tile([P, P], BF16)
        nc.vector.memset(tiny[:], TINY)
        factor_rows = []
        for j in range(2):
            factor_row = const.tile([P, P], F32, name="factor_rows%d" % j)
            nc.gpsimd.memset(factor_row[:], 1.0)
            factor_rows.append(factor_row)

        neigh_tiles = {}
        src_tiles = {}
        both_tiles = {}

        def by_slot(features):
            return features.rearrange("s m d -> (s m) d").rearrange("(g p) d -> p g d", p=P)

        def load(kind, i, pieces=1, queue=nc.sync, part=None):
            features = (src_node_features if kind == "s" else neigh_node_features)[i]
            if on_rows(i):
                tiles = src_tiles if kind == "s" else neigh_tiles
                if i not in tiles:
                    tile = inputs.tile([P, SLOTS, FEAT], BF16, name="%s%d" % (kind, i))
                    tiles[i] = tile
                tile = tiles[i]
                step = SLOTS // pieces
                for m in range(0, SLOTS, step):
                    if part is not None and m // step not in part:
                        continue
                    nc.sync.dma_start(out=tile[:, m : m + step, :], in_=features[:, m : m + step, :])
            else:
                if i not in both_tiles:
                    both = inputs.tile([P, GROUPS, K], BF16, name="both%d" % i)
                    both_tiles[i] = both
                cols = slice(0, FEAT) if kind == "s" else slice(FEAT, K)
                step = GROUPS // pieces
                for g in range(0, GROUPS, step):
                    if part is not None and g // step not in part:
                        continue
                    queue.dma_start(
                        out=both_tiles[i][:, g : g + step, cols], in_=by_slot(features)[:, g : g + step, :]
                    )

        w_words = const.tile([P, PACK * H], U8, align_bytes=64)
        bias_all = const.tile([P, H], BF16)

        def load_small():
            nc.sync.dma_start(out=bias_rows[0:H_BLOCKS, :], in_=b_map.rearrange("(c h) -> c h", c=H_BLOCKS))
            for quadrant in range(4):
                nc.sync.dma_start(
                    out=w_scales[32 * quadrant : 32 * quadrant + 4, :].bitcast(I32),
                    in_=W_map_scales[0, 4 * quadrant : 4 * quadrant + 4, :].bitcast(I32),
                )

        def load_weights():
            nc.sync.dma_start(
                out=w_words[:].bitcast(I32),
                in_=W_map_words[0].rearrange("p n t -> p (n t)").bitcast(I32),
            )

        bias_cols = const.tile([P, H_BLOCKS], BF16)

        bspread_ps = {}

        def bias_to_columns():
            bias_cols_ps = psum.tile([P, H], BF16, name="small", bufs=2)
            nc.tensor.transpose(bias_cols_ps[:, 0:P], bias_rows[:], ident[:])
            nc.vector.tensor_copy(out=bias_cols[:], in_=bias_cols_ps[:, 0:H_BLOCKS])

        def spread_bias():
            bias_ps = psum.tile([P, H], BF16, name="acc", bufs=4)
            for c in range(H_BLOCKS):
                nc.tensor.transpose(
                    bias_ps[:, c * P : (c + 1) * P], bias_cols[:, c : c + 1].to_broadcast([P, P]), ident[:]
                )
            bspread_ps[0] = bias_ps

        def copy_bias():
            nc.scalar.copy(out=bias_all[:], in_=bspread_ps[0][:])

        for item in LOADS.split():
            if item == "small":
                load_small()
            elif item == "w":
                load_weights()
            else:
                load(
                    item[0],
                    int(item[1]),
                    int(item[3]) if len(item) > 2 else 1,
                    part=[int(x) for x in item.split(":")[1]] if ":" in item else None,
                )

        partial_of = {}
        masked_of = {}
        cnt_of = {}
        hidden_of = {}
        alo_of = {}
        or_of = {}
        row_abs_of = {}
        inv_count_of = {}
        factor_of = {}
        small_ps_of = {}
        result_of = {}
        hidden_ps_of = {}
        grouped_of = {}
        codes_of = {}
        acc_of = {}

        def neigh_row(i, r):
            if on_rows(i):
                return neigh_tiles[i][:, r, :]
            return both_tiles[i][:, r, FEAT:K]

        def engine_of(i, which):
            return nc.gpsimd if (i, which) in GPSIMD_TREES else nc.vector

        def chunk_of(i, which):
            return CHUNK if (i, which) in GPSIMD_TREES or (i, which) in HALF_TREES else SLOTS // 4

        def add_quarter(i, which, q):
            tile = (src_tiles if which == 0 else neigh_tiles)[i]
            quarter = SLOTS // 4
            if q == 1:
                tag = "partial%d%s" % (which, "g" if (i, which) in GPSIMD_TREES else "v")
                partial = work.tile([P, quarter, FEAT], F32, name=tag, bufs=3)
                partial_of[(i, which)] = partial
            partial = partial_of[(i, which)]
            for m in range(0, quarter, chunk_of(i, which)):
                engine_of(i, which).tensor_tensor(
                    out=partial[:, m : m + chunk_of(i, which), :],
                    in0=tile[:, q * quarter + m : q * quarter + m + chunk_of(i, which), :],
                    in1=tile[:, m : m + chunk_of(i, which), :] if q == 1 else partial[:, m : m + chunk_of(i, which), :],
                    op=ALU.add,
                )

        def fold(i, which, width):
            partial = partial_of[(i, which)]
            engine_of(i, which).tensor_tensor(
                out=partial[:, 0:width, :],
                in0=partial[:, 0:width, :],
                in1=partial[:, width : 2 * width, :],
                op=ALU.add,
            )

        def tree(i, which):
            for q in (1, 2, 3):
                add_quarter(i, which, q)
            fold(i, which, 2)
            fold(i, which, 1)

        def two_trees(i):
            for q in (1, 2, 3):
                add_quarter(i, 1, q)
            add_quarter(i, 0, 1)
            fold(i, 1, 2)
            add_quarter(i, 0, 2)
            fold(i, 1, 1)
            add_quarter(i, 0, 3)
            fold(i, 0, 2)
            fold(i, 0, 1)

        def test_rows_scalar(i, first, last):
            if first == 0:
                row_abs = work.tile([P, SLOTS], F32, bufs=NODE_TILES)
                row_abs_of[i] = row_abs
            for r in range(first, last):
                unused = work.tile([P, FEAT], BF16)
                nc.scalar.activation(
                    out=unused[:], in_=neigh_row(i, r), func=ACT.Abs, accum_out=row_abs_of[i][:, r : r + 1]
                )

        def invert_count_of_rows(i):
            valid = work.tile([P, SLOTS], F32)
            count = work.tile([P, 1], F32)
            nc.scalar.activation(out=valid[:], in_=row_abs_of[i][:], func=ACT.Sign, accum_out=count[:])
            cnt_of[i] = count

        def test_rows_vector(i, first, last):
            for r in range(first, last):
                nc.vector.tensor_reduce(
                    out=row_abs_of[i][:, r : r + 1],
                    in_=neigh_row(i, r),
                    axis=AX.X,
                    op=ALU.max,
                    apply_absolute_value=True,
                )

        def imax(i):
            at_least_one = work.tile([P, 1], F32)
            nc.vector.tensor_scalar_max(out=at_least_one[:], in0=cnt_of[i][:], scalar1=1.0)
            alo_of[i] = at_least_one

        def irec(i):
            inv_count = const.tile([P, 1], F32, name="inv_count_kept%d" % i)
            nc.vector.reciprocal(out=inv_count[:], in_=alo_of[i][:])
            inv_count_of[i] = inv_count

        def count_on_tensor(i):
            masked = work.tile([P, GROUPS, GROUP], BF16)
            nc.vector.scalar_tensor_tensor(
                out=masked[:],
                in0=row_abs_of[i][:].rearrange("q (g o) -> q g o", o=1).to_broadcast([P, GROUPS, GROUP]),
                scalar=0.0,
                in1=slot_sum[:].rearrange("q (o n) -> q o n", o=1).to_broadcast([P, GROUPS, GROUP]),
                op0=ALU.is_gt,
                op1=ALU.mult,
            )
            masked_of[i] = masked

        def count_matmul(i):
            masked = masked_of[i]
            small_ps = psum.tile([P, N_TILE], F32, name="small", bufs=2)
            nc.tensor.matmul(
                out=small_ps[:, P : P + 1],
                lhsT=masked[:].rearrange("q g n -> q (g n)"),
                rhs=ones_col[:],
                start=True,
                stop=False,
            )
            nc.tensor.matmul(
                out=small_ps[:, P : P + 1], lhsT=tiny[:], rhs=ones_col[:], start=False, stop=True
            )
            small_ps_of[i] = small_ps

        def factor_to_rows(i):
            at_least_one = work.tile([P, 1], F32)
            nc.vector.tensor_scalar_max(out=at_least_one[:], in0=small_ps_of[i][:, P : P + 1], scalar1=1.0)
            alo_of[i] = at_least_one

        def frecip(i):
            inv_count = work.tile([P, 1], F32)
            nc.vector.reciprocal(out=inv_count[:], in_=small_ps_of[i][:, P : P + 1])
            inv_count_of[i] = inv_count

        def fspread(i):
            inv_count = inv_count_of[i]
            nc.vector.tensor_copy(
                out=factor_rows[i % 2][:, SRC_P:P], in_=inv_count[:, 0:1].to_broadcast([P, P - SRC_P])
            )

        def transpose_factor(i):
            nc.tensor.transpose(small_ps_of[i][:, 0:P], factor_rows[i % 2][:], ident_f32[:])

        def copy_factor(i):
            factor = work.tile([P, P], F32, bufs=3)
            (nc.scalar.copy if i in SCALAR_FACTOR else nc.vector.tensor_copy)(out=factor[:], in_=small_ps_of[i][:, 0:P])
            factor_of[i] = factor

        def sum_on_tensor(i, first, last):
            if first == 0:
                hidden_ps = psum.tile([P, PACK, P], F32, bufs=2)
                hidden_ps_of[i] = hidden_ps
            hidden_ps = hidden_ps_of[i]
            for g in range(first, last):
                for t in range(PACK):
                    nc.tensor.matmul(
                        out=hidden_ps[:, t, g * GROUP : (g + 1) * GROUP],
                        lhsT=both_tiles[i][:, g, t:K:PACK],
                        rhs=slot_sum[:],
                        start=True,
                        stop=True,
                    )

        def scale_and_group(i):
            grouped = work.tile([P, P, PACK], BF16, bufs=4, align_bytes=64)
            nc.vector.tensor_tensor(
                out=grouped[:],
                in0=hidden_ps_of[i][:].rearrange("p t n -> p n t"),
                in1=factor_of[i][:].rearrange("p (n o) -> p n o", o=1).to_broadcast([P, P, PACK]),
                op=ALU.mult,
            )
            grouped_of[i] = grouped

        def new_hidden(i):
            if i not in hidden_of:
                hidden = work.tile([P, PACK, P], BF16)
                hidden_of[i] = hidden

        def source_row(i):
            new_hidden(i)
            hidden = hidden_of[i]
            partial = partial_of[(i, 0)]
            nc.vector.tensor_tensor(
                out=hidden[:, :, 0:SRC_P],
                in0=partial[:, 0, :].rearrange("n (p t) -> n t p", t=PACK),
                in1=partial[:, 1, :].rearrange("n (p t) -> n t p", t=PACK),
                op=ALU.add,
            )

        def neigh_row_scalar(i):
            new_hidden(i)
            nc.scalar.activation(
                out=hidden_of[i][:, :, SRC_P:P],
                in_=partial_of[(i, 1)][:, 0, :].rearrange("n (p t) -> n t p", t=PACK),
                func=ACT.Copy,
                scale=inv_count_of[i][:, 0:1],
            )

        def neigh_row_mean(i):
            new_hidden(i)
            nc.vector.tensor_scalar(
                out=hidden_of[i][:, :, SRC_P:P],
                in0=partial_of[(i, 1)][:, 0, :].rearrange("n (p t) -> n t p", t=PACK),
                scalar1=inv_count_of[i][:, 0:1],
                scalar2=None,
                op0=ALU.mult,
            )

        def rows_to_hidden_ps(i):
            hidden = hidden_of[i]
            hidden_t = psum.tile([P, 2 * PACK, P], BF16, name="small", bufs=2)
            for t in range(PACK):
                nc.tensor.transpose(hidden_t[:, t, :], hidden[:, t, :], ident[:])
            hidden_ps_of[i] = hidden_t

        def group_only(i):
            grouped = work.tile([P, P, PACK], BF16, bufs=4, align_bytes=64)
            nc.scalar.copy(out=grouped[:], in_=hidden_ps_of[i][:, 0:PACK, :].rearrange("p t n -> p n t"))
            grouped_of[i] = grouped

        def quantise(i):
            codes = work.tile([P, P], U32, bufs=4, align_bytes=64)
            scales = work.tile([P, P], U8, bufs=4, align_bytes=64)
            nc.vector.quantize_mx(
                out=codes[:].bitcast(FP8X4),
                scales=scales[:],
                in_=grouped_of[i][:].rearrange("p n t -> p (n t)"),
            )
            codes_of[i] = (codes, scales)

        def multiply(i, first=0, last=2):
            codes, scales = codes_of[i]
            if first == 0:
                acc_of[i] = []
            banks = acc_of[i]
            for h in range(first, last):
                acc = psum.tile([P, N_TILE], F32, bufs=4)
                nc.tensor.matmul_mx(
                    out=acc[:],
                    lhsT=codes[:].bitcast(FP8X4),
                    lhsT_scale=scales[:],
                    rhs=w_words[:, h * PACK * N_TILE : (h + 1) * PACK * N_TILE].bitcast(FP8X4),
                    rhs_scale=w_scales[:, h * N_TILE : (h + 1) * N_TILE],
                    start=True,
                    stop=True,
                )
                banks.append(acc)

        def add_bias(i, h):
            if h == 0:
                result = results.tile([P, H], F32)
                result_of[i] = result
            cols = slice(h * N_TILE, (h + 1) * N_TILE)
            nc.vector.tensor_tensor(
                out=result_of[i][:, cols], in0=acc_of[i][h][:], in1=bias_all[:, cols], op=ALU.add
            )

        def leaky_and_store(i, h=None):
            cols = slice(0, H) if h is None else slice(h * N_TILE, (h + 1) * N_TILE)
            result = result_of[i]
            nc.vector.scalar_tensor_tensor(
                out=result[:, cols],
                in0=result[:, cols],
                scalar=NEG_SLOPE,
                in1=result[:, cols],
                op0=ALU.mult,
                op1=ALU.max,
            )
            if i in FULL_STORE:
                if h != 0:
                    nc.sync.dma_start(out=out[i * P : (i + 1) * P, :], in_=result[:])
            else:
                nc.sync.dma_start(out=out[i * P : (i + 1) * P, cols], in_=result[:, cols])

        def leaky_piece(i, q):
            cols = slice(q * FEAT, (q + 1) * FEAT)
            result = result_of[i]
            nc.vector.scalar_tensor_tensor(
                out=result[:, cols], in0=result[:, cols], scalar=NEG_SLOPE, in1=result[:, cols], op0=ALU.mult, op1=ALU.max
            )
            nc.sync.dma_start(out=out[i * P : (i + 1) * P, cols], in_=result[:, cols])

        def gleaky(i, h=None):
            cols = slice(0, H) if h is None else slice(h * N_TILE, (h + 1) * N_TILE)
            result = result_of[i]
            below = work.tile([P, H], F32, bufs=1)
            nc.gpsimd.tensor_scalar(
                out=below[:, cols], in0=result[:, cols], scalar1=0.0, scalar2=NEG_SLOPE - 1.0, op0=ALU.min, op1=ALU.mult
            )
            nc.gpsimd.tensor_tensor(out=result[:, cols], in0=result[:, cols], in1=below[:, cols], op=ALU.add)
            nc.sync.dma_start(out=out[i * P : (i + 1) * P, cols], in_=result[:, cols])

        def finish(i):
            add_bias(i, 0)
            add_bias(i, 1)
            leaky_and_store(i, 0)
            leaky_and_store(i, 1)

        verbs = {
            "tests": test_rows_scalar,
            "vtests": test_rows_vector,
            "ssrc": lambda i, pieces: load("s", i, pieces, nc.scalar),
            "gsrc": lambda i, pieces: load("s", i, pieces, nc.gpsimd),
            "trees": two_trees,
            "quarter": add_quarter,
            "fold": fold,
            "tree": tree,
            "sgn": invert_count_of_rows,
            "imax": imax,
            "irec": irec,
            "srow": source_row,
            "nrow": neigh_row_mean,
            "nrowA": neigh_row_scalar,
            "leaky2": leaky_piece,
            "rows": rows_to_hidden_ps,
            "group": group_only,
            "quant": quantise,
            "mul": multiply,
            "mask": count_on_tensor,
            "cnt": count_matmul,
            "fmax": factor_to_rows,
            "frecip": frecip,
            "fspread": fspread,
            "ft": transpose_factor,
            "fcopy": copy_factor,
            "sum": sum_on_tensor,
            "scale": scale_and_group,
            "add": add_bias,
            "leaky": leaky_and_store,
            "gleaky": gleaky,
            "bcols": bias_to_columns,
            "bspread": spread_bias,
            "bcopy": copy_bias,
        }
        with tc.manual_schedule():
            for word in ORDER.split():
                parts = word.split(":")
                verbs[parts[0]](*[int(x) for part in parts[1:] for x in part.split(",")])
